import numpy as np
import ml_dtypes


def mxq(x, axis, fmt="e4m3"):
    dtype, down = {"e4m3": (ml_dtypes.float8_e4m3fn, 7), "e5m2": (ml_dtypes.float8_e5m2, 14)}[fmt]
    v = np.moveaxis(np.asarray(x, np.float32).astype(ml_dtypes.bfloat16).astype(np.float64), axis, -1)
    blocks = v.reshape(v.shape[:-1] + (-1, 32))
    amax = np.abs(blocks).max(-1, keepdims=True)
    byte = np.maximum(np.where(amax > 0, np.frexp(amax)[1] - 1 + 127, 0) - down, 1)
    scale = np.exp2(byte - 127.0)
    codes = (blocks / scale).astype(np.float32).astype(dtype).astype(np.float64)
    return np.moveaxis((codes * scale).reshape(v.shape), -1, axis)


WIDE = False


def mx_kscale(k):
    if not WIDE:
        return np.ones(k)
    levels = np.array([10, -10, 5, -5, 0])
    a = np.random.permutation(np.resize(levels, k // 512 * 4)).reshape(k // 512, 4)
    idx = np.arange(k)
    return np.exp2(a[idx // 512, idx % 128 // 32])


BF16 = ml_dtypes.bfloat16


def bf(x):
    return np.asarray(x, np.float32).astype(BF16)


def f64(x):
    return np.asarray(x).astype(np.float64)


E2M1 = np.array([0.0, 0.5, 1.0, 1.5, 2.0, 3.0, 4.0, 6.0, -0.0, -0.5, -1.0, -1.5, -2.0, -3.0, -4.0, -6.0])


def pack_weight(w, fmt):
    k, n = w.shape
    w = f64(bf(w)).reshape(k // 32, 32, n)
    amax = np.abs(w).max(1)
    if fmt == "e4m3":
        byte = np.frexp(amax)[1] - 1 + 127 - 7
    else:
        mant, ex = np.frexp(amax / 6.0)
        byte = np.where(mant > 0.5, ex, ex - 1) + 127
    byte = np.clip(np.where(amax > 0, byte, 1), 1, 254)
    scaled = (w * np.exp2(127.0 - byte)[:, None, :]).reshape(k, n).astype(np.float32)
    by_word = np.ascontiguousarray(scaled.reshape(k // 512, 128, 4, n).transpose(0, 1, 3, 2))
    if fmt == "e4m3":
        words = by_word.astype(ml_dtypes.float8_e4m3fn).view(np.uint8)
    else:
        c = by_word.astype(ml_dtypes.float4_e2m1fn).view(np.uint8) & 0xF
        words = c[..., 0::2] | (c[..., 1::2] << 4)
    return np.ascontiguousarray(words), np.ascontiguousarray(byte.astype(np.uint8).reshape(k // 512, 16, n))


def unpack_weight(words, scales, fmt):
    g, p, n, _ = words.shape
    if fmt == "e4m3":
        vals = np.ascontiguousarray(words).view(ml_dtypes.float8_e4m3fn).astype(np.float64)
    else:
        nib = np.empty((g, p, n, 4), np.uint8)
        nib[..., 0::2] = words & 0xF
        nib[..., 1::2] = words >> 4
        vals = E2M1[nib]
    vals = vals * np.repeat(np.exp2(scales.astype(np.float64) - 127.0), 8, axis=1)[..., None]
    return vals.transpose(0, 1, 3, 2).reshape(g * 512, n)

def pack4(w):
    words, scales = pack_weight(w, "e2m1")
    return words.reshape(words.shape[0], 128, -1), scales


def unpack4(words, scales):
    return unpack_weight(words.reshape(words.shape[0], 128, -1, 2), scales, "e2m1")


N, DIN, DHID, DOUT, DMLP, NF = 256, 1024, 2048, 512, 512, 8
G = 3 * DHID
FS = N // NF
SYNC = 0.15


def sigmoid(v):
    return 1.0 / (1.0 + np.exp(-v))


def setup_inputs():
    s = mx_kscale(DOUT)
    o = np.random.standard_normal((N, DOUT)) * (0.8 + 0.8 * np.random.random((N, 1)))
    rows = np.concatenate([0.55 / np.sqrt(DOUT) / s, np.array([0.3])])
    eng_out = bf(o * s)
    tension = bf((o * o).mean(-1))
    hiddens = bf(np.random.standard_normal((N, DHID)) * (0.5 + np.random.random((N, 1))))
    w_ih = bf(np.random.standard_normal((DOUT + 1, G)) * rows[:, None])
    b_ih = bf(np.random.standard_normal(G) * 0.3)
    w_hh_words, w_hh_scales = pack4(np.random.standard_normal((DHID, G)) * 0.7 / np.sqrt(DHID))
    b_hh = bf(np.random.standard_normal(G) * 0.3)
    return {
        "eng_out": eng_out,
        "tension": tension,
        "hiddens": hiddens,
        "w_ih": w_ih,
        "b_ih": b_ih,
        "w_hh_words": w_hh_words,
        "w_hh_scales": w_hh_scales,
        "b_hh": b_hh,
    }


def reference(eng_out, tension, hiddens, w_ih, b_ih, w_hh_words, w_hh_scales, b_hh):
    h = f64(hiddens)
    wi = f64(w_ih)
    gi = (mxq(f64(eng_out), 1, "e4m3") @ mxq(wi[:DOUT], 0, "e4m3")) + f64(tension)[:, None] * wi[DOUT] + f64(b_ih)
    gh = (mxq(h, 1, "e4m3") @ unpack4(w_hh_words, w_hh_scales)) + f64(b_hh)
    ir, iz, inn = np.split(gi, 3, axis=-1)
    hr, hz, hn = np.split(gh, 3, axis=-1)
    r = sigmoid(ir + hr)
    z = sigmoid(iz + hz)
    ncand = np.tanh(inn + r * hn)
    h_new = (1.0 - z) * ncand + z * h
    hf = h_new.reshape(NF, FS, DHID)
    fmean = hf.mean(axis=1, keepdims=True)
    hf = (1.0 - SYNC) * hf + SYNC * fmean
    return hf.reshape(N, DHID)

@@ -1,0 +1,296 @@
+from contextlib import ExitStack
+
+import concourse.mybir as mybir
+from concourse.masks import make_identity
+
+F32 = mybir.dt.float32
+BF16 = mybir.dt.bfloat16
+I32 = mybir.dt.int32
+U32 = mybir.dt.uint32
+U8 = mybir.dt.uint8
+FP8X4 = mybir.dt.float8_e4m3fn_x4
+FP4X4 = mybir.dt.float4_e2m1fn_x4
+ALU = mybir.AluOpType
+ACT = mybir.ActivationFunctionType
+
+P = 128
+PACK = 4
+K_PASS = P * PACK
+CELLS = 256
+ROW_TILES = CELLS // P
+D_IN = 512
+D_HID = 2048
+HID_PASSES = D_HID // K_PASS
+GATES = 3
+R = 0
+Z = 1
+N = 2
+CHUNK = 512
+CHUNKS = D_HID // CHUNK
+FACTION = 32
+
+GATE_ORDER = (R, N, Z)
+HALVES = ((R, 0), (R, 1), (N, 0), (N, 1), (Z, 0), (Z, 1))
+
+FLOPS = 2 * CELLS * GATES * D_HID * (D_IN + D_HID)
+
+
+def tile_fractalengine_pb_kernel(
+    tc, eng_out, tension, hiddens, w_ih, b_ih, w_hh_words, w_hh_scales, b_hh, out
+):
+    nc = tc.nc
+
+    def gate_cols(gate, c):
+        return slice(gate * D_HID + c * CHUNK, gate * D_HID + (c + 1) * CHUNK)
+
+    def row_tile(i):
+        return slice(i * P, (i + 1) * P)
+
+    with ExitStack() as ctx:
+        keep = ctx.enter_context(tc.tile_pool(name="keep", bufs=1))
+        stream = ctx.enter_context(tc.tile_pool(name="stream", bufs=1))
+        work = ctx.enter_context(tc.tile_pool(name="work", bufs=3))
+        psum = ctx.enter_context(tc.psum_pool(name="psum", bufs=1))
+
+        def bank(shape, tag):
+            return psum.tile(shape, F32, name=tag, tag=tag, bufs=6 if tag == "acc" else 2)
+
+        h_sb = keep.tile([P, ROW_TILES, D_HID], BF16)
+        eng_sb = keep.tile([P, ROW_TILES, D_IN], BF16)
+        h_codes = keep.tile([P, HID_PASSES, CELLS], U32, align_bytes=64)
+        h_scales = keep.tile([P, HID_PASSES, CELLS], U8, align_bytes=64)
+        eng_codes = keep.tile([P, 1, CELLS], U32, align_bytes=64)
+        eng_scales = keep.tile([P, 1, CELLS], U8, align_bytes=64)
+        wh_scales = keep.tile([P, HID_PASSES, GATES * D_HID], U8, align_bytes=64)
+        ident = keep.tile([P, P], F32)
+        mix = keep.tile([P, P], F32)
+        left = keep.tile([P, ROW_TILES + 1, P], BF16)
+        rows = keep.tile([P, GATES * D_HID], BF16)
+
+        w_ih_packed = w_ih[0:D_IN, :].rearrange("(p j) n -> p j n", j=PACK)
+        words_i32 = w_hh_words.bitcast(I32).rearrange("g p n -> p g n")
+        scales_i32 = w_hh_scales.bitcast(I32).rearrange("g q n -> q g n")
+        raw = {}
+        words = {}
+
+        def load_scale_rows(gate):
+            cols = slice(gate * D_HID, (gate + 1) * D_HID)
+            nc.vector.memset(wh_scales[:, :, cols].bitcast(I32), 0)
+            for half in range(2):
+                for r4 in range(4):
+                    q = 4 * half + r4
+                    nc.sync.dma_start(
+                        out=wh_scales[32 * half + r4 : P : 64, :, cols].bitcast(I32),
+                        in_=scales_i32[q : 16 : 8, :, gate * D_HID // 4 : (gate + 1) * D_HID // 4],
+                    )
+
+        def load_chunk(c):
+            for gate in GATE_ORDER:
+                raw[c, gate] = stream.tile([P, PACK, CHUNK], BF16, name="raw", tag="raw", bufs=6)
+                nc.sync.dma_start(out=raw[c, gate][:], in_=w_ih_packed[:, :, gate_cols(gate, c)])
+                if c == 0:
+                    load_scale_rows(gate)
+                words[c, gate] = stream.tile(
+                    [P, HID_PASSES, 2 * CHUNK], U8, name="words", tag="words", bufs=9, align_bytes=64
+                )
+                first = (gate * D_HID + c * CHUNK) // 2
+                nc.sync.dma_start(
+                    out=words[c, gate][:].bitcast(I32), in_=words_i32[:, :, first : first + CHUNK // 2]
+                )
+
+        grouped = {}
+        wi_codes = {}
+        wi_scales = {}
+
+        def half_cols(half):
+            return slice(half * CHUNK // 2, (half + 1) * CHUNK // 2)
+
+        def regroup(c, gate, half):
+            grouped[c, gate, half] = stream.tile(
+                [P, CHUNK // 2, PACK], BF16, name="grouped", tag="grouped", bufs=6, align_bytes=64
+            )
+            nc.scalar.copy(
+                out=grouped[c, gate, half][:].rearrange("p (c i) j -> p c j i", i=4),
+                in_=raw[c, gate][:, :, half_cols(half)].rearrange("p j (c i) -> p c j i", i=4),
+            )
+
+        def quantise(c, gate, half):
+            if half == 0:
+                wi_codes[c, gate] = stream.tile(
+                    [P, CHUNK], U32, name="wi_codes", tag="wi_codes", bufs=6, align_bytes=64
+                )
+                wi_scales[c, gate] = stream.tile(
+                    [P, CHUNK], U8, name="wi_scales", tag="wi_scales", bufs=6, align_bytes=64
+                )
+            nc.vector.quantize_mx(
+                out=wi_codes[c, gate][:, half_cols(half)].bitcast(FP8X4),
+                scales=wi_scales[c, gate][:, half_cols(half)],
+                in_=grouped[c, gate, half][:].rearrange("p w j -> p (w j)"),
+            )
+
+        def hidden_passes(acc, c, i, gate, stop):
+            for g in range(HID_PASSES):
+                nc.tensor.matmul_mx(
+                    out=acc[:],
+                    lhsT=h_codes[:, g, row_tile(i)].bitcast(FP8X4),
+                    lhsT_scale=h_scales[:, g, row_tile(i)],
+                    rhs=words[c, gate][:, g, :].bitcast(FP4X4),
+                    rhs_scale=wh_scales[:, g, gate_cols(gate, c)],
+                    start=g == 0,
+                    stop=stop and g == HID_PASSES - 1,
+                )
+
+        def input_pass(acc, c, i, gate, start):
+            nc.tensor.matmul_mx(
+                out=acc[:],
+                lhsT=eng_codes[:, 0, row_tile(i)].bitcast(FP8X4),
+                lhsT_scale=eng_scales[:, 0, row_tile(i)],
+                rhs=wi_codes[c, gate][:].bitcast(FP8X4),
+                rhs_scale=wi_scales[c, gate][:],
+                start=start,
+                stop=True,
+            )
+
+        def plain_terms(acc, which, c, gate):
+            nc.tensor.matmul(
+                out=acc[:], lhsT=left[:, which, :], rhs=rows[:, gate_cols(gate, c)], start=True, stop=True
+            )
+
+        gate_sb = {}
+        hid_bias = {}
+        cand = {}
+        h_new = {}
+
+        def prepare_plain_terms(c, i):
+            for gate in (R, Z):
+                acc = bank([P, CHUNK], "acc")
+                plain_terms(acc, i, c, gate)
+                gate_sb[c, i, gate] = work.tile([P, CHUNK], F32, name="gate_sb", tag="gate_sb", bufs=8)
+                nc.scalar.copy(out=gate_sb[c, i, gate][:], in_=acc[:])
+            if i == 0:
+                acc = bank([P, CHUNK], "acc")
+                plain_terms(acc, ROW_TILES, c, N)
+                hid_bias[c] = work.tile([P, CHUNK], F32, name="hid_bias", tag="hid_bias", bufs=3)
+                nc.scalar.copy(out=hid_bias[c][:], in_=acc[:])
+
+        def sigmoid_gate(c, i, gate):
+            acc = bank([P, CHUNK], "acc")
+            hidden_passes(acc, c, i, gate, stop=False)
+            input_pass(acc, c, i, gate, start=False)
+            nc.vector.tensor_add(out=gate_sb[c, i, gate][:], in0=acc[:], in1=gate_sb[c, i, gate][:])
+            nc.scalar.activation(out=gate_sb[c, i, gate][:], in_=gate_sb[c, i, gate][:], func=ACT.Sigmoid)
+
+        def candidate(c, i):
+            cand[c, i] = work.tile([P, CHUNK], F32, name="cand", tag="cand")
+            acc = bank([P, CHUNK], "acc")
+            hidden_passes(acc, c, i, N, stop=True)
+            nc.vector.tensor_add(out=cand[c, i][:], in0=acc[:], in1=hid_bias[c][:])
+            nc.vector.tensor_mul(out=cand[c, i][:], in0=cand[c, i][:], in1=gate_sb[c, i, R][:])
+            acc = bank([P, CHUNK], "acc")
+            input_pass(acc, c, i, N, start=True)
+            nc.vector.tensor_add(out=cand[c, i][:], in0=acc[:], in1=cand[c, i][:])
+            acc = bank([P, CHUNK], "acc")
+            plain_terms(acc, i, c, N)
+            nc.vector.tensor_add(out=cand[c, i][:], in0=acc[:], in1=cand[c, i][:])
+            nc.scalar.activation(out=cand[c, i][:], in_=cand[c, i][:], func=ACT.Tanh)
+
+        def blend(c, i):
+            h_new[c, i] = work.tile([P, CHUNK], F32, name="h_new", tag="h_new")
+            nc.vector.tensor_sub(
+                out=h_new[c, i][:], in0=h_sb[:, i, c * CHUNK : (c + 1) * CHUNK], in1=cand[c, i][:]
+            )
+            nc.vector.tensor_mul(out=h_new[c, i][:], in0=h_new[c, i][:], in1=gate_sb[c, i, Z][:])
+            nc.vector.tensor_add(out=h_new[c, i][:], in0=h_new[c, i][:], in1=cand[c, i][:])
+
+        def mix_and_store(c, i):
+            mixed = bank([P, CHUNK], "mix")
+            nc.tensor.matmul(out=mixed[:], lhsT=mix[:], rhs=h_new[c, i][:], start=True, stop=True)
+            result = work.tile([P, CHUNK], F32)
+            nc.scalar.mul(out=result[:], in_=mixed[:], mul=0.05 / FACTION)
+            nc.scalar.dma_start(out=out[row_tile(i), c * CHUNK : (c + 1) * CHUNK], in_=result[:])
+
+        for i in range(ROW_TILES):
+            nc.sync.dma_start(out=h_sb[:, i, :], in_=hiddens[row_tile(i), :])
+        for i in range(ROW_TILES):
+            nc.sync.dma_start(out=eng_sb[:, i, :], in_=eng_out[row_tile(i), :])
+
+        nc.vector.memset(rows[:].bitcast(I32), 0)
+        nc.vector.memset(left[:].bitcast(I32), 0)
+        nc.vector.memset(left[32:33, 0:ROW_TILES, :], 1.0)
+        nc.vector.memset(left[64:65, 0:ROW_TILES, :], 1.0)
+        nc.vector.memset(left[96:97, ROW_TILES, :], 1.0)
+        nc.sync.dma_start(out=rows[0:1, :], in_=w_ih[D_IN : D_IN + 1, :])
+        nc.sync.dma_start(out=rows[32:33, :], in_=b_ih.rearrange("(o n) -> o n", o=1))
+        b_hh_row = b_hh.rearrange("(o n) -> o n", o=1)
+        nc.sync.dma_start(out=rows[64:65, 0 : N * D_HID], in_=b_hh_row[:, 0 : N * D_HID])
+        nc.sync.dma_start(out=rows[96:97, N * D_HID :], in_=b_hh_row[:, N * D_HID :])
+        nc.sync.dma_start(
+            out=left[0:1, 0:ROW_TILES, :], in_=tension.rearrange("(o i r) -> o i r", o=1, i=ROW_TILES)
+        )
+
+        load_chunk(0)
+        load_chunk(1)
+
+        make_identity(nc, ident[:])
+        nc.vector.memset(mix[:], 0.0)
+        for f in range(P // FACTION):
+            block = slice(f * FACTION, (f + 1) * FACTION)
+            nc.vector.memset(mix[block, block], 3.0)
+        nc.vector.scalar_tensor_tensor(
+            out=mix[:], in0=ident[:], scalar=544.0, in1=mix[:], op0=ALU.mult, op1=ALU.add
+        )
+
+        def transpose_and_quantise(x_sb, passes, codes, scales):
+            x_words = x_sb[:].bitcast(F32)
+            for g in range(passes):
+                flipped = bank([P, 2, CELLS], "acc")
+                for i in range(ROW_TILES):
+                    for u in range(2):
+                        nc.tensor.transpose(
+                            flipped[:, u, row_tile(i)],
+                            x_words[:, i, K_PASS // 2 * g + u : K_PASS // 2 * (g + 1) : 2],
+                            ident[:],
+                        )
+                x_grouped = stream.tile(
+                    [P, CELLS, PACK], BF16, name="x_grouped", tag="grouped", bufs=6, align_bytes=64
+                )
+                nc.vector.tensor_copy(
+                    out=x_grouped[:].bitcast(F32), in_=flipped[:].rearrange("p u r -> p r u")
+                )
+                nc.vector.quantize_mx(
+                    out=codes[:, g, :].bitcast(FP8X4),
+                    scales=scales[:, g, :],
+                    in_=x_grouped[:].rearrange("p r t -> p (r t)"),
+                )
+
+        transpose_and_quantise(h_sb, HID_PASSES, h_codes, h_scales)
+        transpose_and_quantise(eng_sb, 1, eng_codes, eng_scales)
+
+        for i in range(ROW_TILES):
+            prepare_plain_terms(0, i)
+        for gate, half in HALVES:
+            regroup(0, gate, half)
+            quantise(0, gate, half)
+
+        before = None
+        for c in range(CHUNKS):
+            for i in range(ROW_TILES):
+                ahead = HALVES[3 * i : 3 * i + 3] if c + 1 < CHUNKS else []
+                if i == 0 and c + 2 < CHUNKS:
+                    load_chunk(c + 2)
+                sigmoid_gate(c, i, R)
+                for gate, half in ahead:
+                    regroup(c + 1, gate, half)
+                if before is not None:
+                    blend(*before)
+                candidate(c, i)
+                for gate, half in ahead:
+                    quantise(c + 1, gate, half)
+                sigmoid_gate(c, i, Z)
+                if before is not None:
+                    mix_and_store(*before)
+                if c + 1 < CHUNKS:
+                    prepare_plain_terms(c + 1, i)
+                before = (c, i)
+        blend(*before)
+        mix_and_store(*before)

@@ -196,11 +196,11 @@ def tile_fractalengine_pb_kernel(
 
         def blend(c, i):
             h_new[c, i] = work.tile([P, CHUNK], F32, name="h_new", tag="h_new")
-            nc.vector.tensor_sub(
+            nc.gpsimd.tensor_sub(
                 out=h_new[c, i][:], in0=h_sb[:, i, c * CHUNK : (c + 1) * CHUNK], in1=cand[c, i][:]
             )
-            nc.vector.tensor_mul(out=h_new[c, i][:], in0=h_new[c, i][:], in1=gate_sb[c, i, Z][:])
-            nc.vector.tensor_add(out=h_new[c, i][:], in0=h_new[c, i][:], in1=cand[c, i][:])
+            nc.gpsimd.tensor_mul(out=h_new[c, i][:], in0=h_new[c, i][:], in1=gate_sb[c, i, Z][:])
+            nc.gpsimd.tensor_add(out=h_new[c, i][:], in0=h_new[c, i][:], in1=cand[c, i][:])
 
         def mix_and_store(c, i):
             mixed = bank([P, CHUNK], "mix")

@@ -30,7 +30,6 @@ CHUNKS = D_HID // CHUNK
 FACTION = 32
 
 GATE_ORDER = (R, N, Z)
-HALVES = ((R, 0), (R, 1), (N, 0), (N, 1), (Z, 0), (Z, 1))
 
 FLOPS = 2 * CELLS * GATES * D_HID * (D_IN + D_HID)
 
@@ -49,7 +48,7 @@ def tile_fractalengine_pb_kernel(
     with ExitStack() as ctx:
         keep = ctx.enter_context(tc.tile_pool(name="keep", bufs=1))
         stream = ctx.enter_context(tc.tile_pool(name="stream", bufs=1))
-        work = ctx.enter_context(tc.tile_pool(name="work", bufs=3))
+        work = ctx.enter_context(tc.tile_pool(name="work", bufs=4))
         psum = ctx.enter_context(tc.psum_pool(name="psum", bufs=1))
 
         def bank(shape, tag):
@@ -66,6 +65,8 @@ def tile_fractalengine_pb_kernel(
         mix = keep.tile([P, P], F32)
         left = keep.tile([P, ROW_TILES + 1, P], BF16)
         rows = keep.tile([P, GATES * D_HID], BF16)
+        rz = keep.tile([P, 2, CHUNKS, ROW_TILES, CHUNK], F32)
+        hid_bias = keep.tile([P, CHUNKS, CHUNK], F32)
 
         w_ih_packed = w_ih[0:D_IN, :].rearrange("(p j) n -> p j n", j=PACK)
         words_i32 = w_hh_words.bitcast(I32).rearrange("g p n -> p g n")
@@ -75,7 +76,6 @@ def tile_fractalengine_pb_kernel(
 
         def load_scale_rows(gate):
             cols = slice(gate * D_HID, (gate + 1) * D_HID)
-            nc.vector.memset(wh_scales[:, :, cols].bitcast(I32), 0)
             for half in range(2):
                 for r4 in range(4):
                     q = 4 * half + r4
@@ -88,6 +88,7 @@ def tile_fractalengine_pb_kernel(
             for gate in GATE_ORDER:
                 raw[c, gate] = stream.tile([P, PACK, CHUNK], BF16, name="raw", tag="raw", bufs=6)
                 nc.sync.dma_start(out=raw[c, gate][:], in_=w_ih_packed[:, :, gate_cols(gate, c)])
+            for gate in GATE_ORDER:
                 if c == 0:
                     load_scale_rows(gate)
                 words[c, gate] = stream.tile(
@@ -105,28 +106,29 @@ def tile_fractalengine_pb_kernel(
         def half_cols(half):
             return slice(half * CHUNK // 2, (half + 1) * CHUNK // 2)
 
-        def regroup(c, gate, half):
-            grouped[c, gate, half] = stream.tile(
-                [P, CHUNK // 2, PACK], BF16, name="grouped", tag="grouped", bufs=6, align_bytes=64
-            )
-            nc.scalar.copy(
-                out=grouped[c, gate, half][:].rearrange("p (c i) j -> p c j i", i=4),
-                in_=raw[c, gate][:, :, half_cols(half)].rearrange("p j (c i) -> p c j i", i=4),
-            )
+        def regroup(c, gate):
+            for half in range(2):
+                grouped[c, gate, half] = stream.tile(
+                    [P, CHUNK // 2, PACK], BF16, name="grouped", tag="grouped", bufs=6, align_bytes=64
+                )
+                nc.scalar.copy(
+                    out=grouped[c, gate, half][:].rearrange("p (c i) j -> p c j i", i=4),
+                    in_=raw[c, gate][:, :, half_cols(half)].rearrange("p j (c i) -> p c j i", i=4),
+                )
 
-        def quantise(c, gate, half):
-            if half == 0:
-                wi_codes[c, gate] = stream.tile(
-                    [P, CHUNK], U32, name="wi_codes", tag="wi_codes", bufs=6, align_bytes=64
-                )
-                wi_scales[c, gate] = stream.tile(
-                    [P, CHUNK], U8, name="wi_scales", tag="wi_scales", bufs=6, align_bytes=64
-                )
-            nc.vector.quantize_mx(
-                out=wi_codes[c, gate][:, half_cols(half)].bitcast(FP8X4),
-                scales=wi_scales[c, gate][:, half_cols(half)],
-                in_=grouped[c, gate, half][:].rearrange("p w j -> p (w j)"),
+        def quantise(c, gate):
+            wi_codes[c, gate] = stream.tile(
+                [P, CHUNK], U32, name="wi_codes", tag="wi_codes", bufs=6, align_bytes=64
             )
+            wi_scales[c, gate] = stream.tile(
+                [P, CHUNK], U8, name="wi_scales", tag="wi_scales", bufs=6, align_bytes=64
+            )
+            for half in range(2):
+                nc.vector.quantize_mx(
+                    out=wi_codes[c, gate][:, half_cols(half)].bitcast(FP8X4),
+                    scales=wi_scales[c, gate][:, half_cols(half)],
+                    in_=grouped[c, gate, half][:].rearrange("p w j -> p (w j)"),
+                )
 
         def hidden_passes(acc, c, i, gate, stop):
             for g in range(HID_PASSES):
@@ -156,36 +158,24 @@ def tile_fractalengine_pb_kernel(
                 out=acc[:], lhsT=left[:, which, :], rhs=rows[:, gate_cols(gate, c)], start=True, stop=True
             )
 
-        gate_sb = {}
-        hid_bias = {}
         cand = {}
         h_new = {}
-
-        def prepare_plain_terms(c, i):
-            for gate in (R, Z):
-                acc = bank([P, CHUNK], "acc")
-                plain_terms(acc, i, c, gate)
-                gate_sb[c, i, gate] = work.tile([P, CHUNK], F32, name="gate_sb", tag="gate_sb", bufs=8)
-                nc.scalar.copy(out=gate_sb[c, i, gate][:], in_=acc[:])
-            if i == 0:
-                acc = bank([P, CHUNK], "acc")
-                plain_terms(acc, ROW_TILES, c, N)
-                hid_bias[c] = work.tile([P, CHUNK], F32, name="hid_bias", tag="hid_bias", bufs=3)
-                nc.scalar.copy(out=hid_bias[c][:], in_=acc[:])
 
         def sigmoid_gate(c, i, gate):
             acc = bank([P, CHUNK], "acc")
             hidden_passes(acc, c, i, gate, stop=False)
             input_pass(acc, c, i, gate, start=False)
-            nc.vector.tensor_add(out=gate_sb[c, i, gate][:], in0=acc[:], in1=gate_sb[c, i, gate][:])
-            nc.scalar.activation(out=gate_sb[c, i, gate][:], in_=gate_sb[c, i, gate][:], func=ACT.Sigmoid)
+            nc.vector.tensor_add(out=rz[:, gate, c, i, :], in0=acc[:], in1=rz[:, gate, c, i, :])
+            nc.scalar.activation(out=rz[:, gate, c, i, :], in_=rz[:, gate, c, i, :], func=ACT.Sigmoid)
 
-        def candidate(c, i):
+        def hidden_part(c, i):
             cand[c, i] = work.tile([P, CHUNK], F32, name="cand", tag="cand")
             acc = bank([P, CHUNK], "acc")
             hidden_passes(acc, c, i, N, stop=True)
-            nc.vector.tensor_add(out=cand[c, i][:], in0=acc[:], in1=hid_bias[c][:])
-            nc.vector.tensor_mul(out=cand[c, i][:], in0=cand[c, i][:], in1=gate_sb[c, i, R][:])
+            nc.vector.tensor_add(out=cand[c, i][:], in0=acc[:], in1=hid_bias[:, c, :])
+
+        def candidate(c, i):
+            nc.vector.tensor_mul(out=cand[c, i][:], in0=cand[c, i][:], in1=rz[:, R, c, i, :])
             acc = bank([P, CHUNK], "acc")
             input_pass(acc, c, i, N, start=True)
             nc.vector.tensor_add(out=cand[c, i][:], in0=acc[:], in1=cand[c, i][:])
@@ -196,11 +186,11 @@ def tile_fractalengine_pb_kernel(
 
         def blend(c, i):
             h_new[c, i] = work.tile([P, CHUNK], F32, name="h_new", tag="h_new")
-            nc.gpsimd.tensor_sub(
+            nc.vector.tensor_sub(
                 out=h_new[c, i][:], in0=h_sb[:, i, c * CHUNK : (c + 1) * CHUNK], in1=cand[c, i][:]
             )
-            nc.gpsimd.tensor_mul(out=h_new[c, i][:], in0=h_new[c, i][:], in1=gate_sb[c, i, Z][:])
-            nc.gpsimd.tensor_add(out=h_new[c, i][:], in0=h_new[c, i][:], in1=cand[c, i][:])
+            nc.vector.tensor_mul(out=h_new[c, i][:], in0=h_new[c, i][:], in1=rz[:, Z, c, i, :])
+            nc.vector.tensor_add(out=h_new[c, i][:], in0=h_new[c, i][:], in1=cand[c, i][:])
 
         def mix_and_store(c, i):
             mixed = bank([P, CHUNK], "mix")
@@ -209,16 +199,18 @@ def tile_fractalengine_pb_kernel(
             nc.scalar.mul(out=result[:], in_=mixed[:], mul=0.05 / FACTION)
             nc.scalar.dma_start(out=out[row_tile(i), c * CHUNK : (c + 1) * CHUNK], in_=result[:])
 
-        for i in range(ROW_TILES):
-            nc.sync.dma_start(out=h_sb[:, i, :], in_=hiddens[row_tile(i), :])
-        for i in range(ROW_TILES):
-            nc.sync.dma_start(out=eng_sb[:, i, :], in_=eng_out[row_tile(i), :])
-
         nc.vector.memset(rows[:].bitcast(I32), 0)
         nc.vector.memset(left[:].bitcast(I32), 0)
         nc.vector.memset(left[32:33, 0:ROW_TILES, :], 1.0)
         nc.vector.memset(left[64:65, 0:ROW_TILES, :], 1.0)
         nc.vector.memset(left[96:97, ROW_TILES, :], 1.0)
+        nc.vector.memset(wh_scales[:].bitcast(I32), 0)
+        make_identity(nc, ident[:])
+
+        for i in range(ROW_TILES):
+            nc.sync.dma_start(out=h_sb[:, i, :], in_=hiddens[row_tile(i), :])
+        for i in range(ROW_TILES):
+            nc.sync.dma_start(out=eng_sb[:, i, :], in_=eng_out[row_tile(i), :])
         nc.sync.dma_start(out=rows[0:1, :], in_=w_ih[D_IN : D_IN + 1, :])
         nc.sync.dma_start(out=rows[32:33, :], in_=b_ih.rearrange("(o n) -> o n", o=1))
         b_hh_row = b_hh.rearrange("(o n) -> o n", o=1)
@@ -227,11 +219,9 @@ def tile_fractalengine_pb_kernel(
         nc.sync.dma_start(
             out=left[0:1, 0:ROW_TILES, :], in_=tension.rearrange("(o i r) -> o i r", o=1, i=ROW_TILES)
         )
-
         load_chunk(0)
         load_chunk(1)
 
-        make_identity(nc, ident[:])
         nc.vector.memset(mix[:], 0.0)
         for f in range(P // FACTION):
             block = slice(f * FACTION, (f + 1) * FACTION)
@@ -239,6 +229,18 @@ def tile_fractalengine_pb_kernel(
         nc.vector.scalar_tensor_tensor(
             out=mix[:], in0=ident[:], scalar=544.0, in1=mix[:], op0=ALU.mult, op1=ALU.add
         )
+
+        for c in range(CHUNKS):
+            for gate in (R, Z):
+                acc = bank([P, CHUNK], "acc")
+                plain_terms(acc, 0, c, gate)
+                nc.scalar.copy(out=rz[:, gate, c, 0, :], in_=acc[:])
+                acc = bank([P, CHUNK], "acc")
+                plain_terms(acc, 1, c, gate)
+                nc.vector.tensor_copy(out=rz[:, gate, c, 1, :], in_=acc[:])
+            acc = bank([P, CHUNK], "acc")
+            plain_terms(acc, ROW_TILES, c, N)
+            nc.scalar.copy(out=hid_bias[:, c, :], in_=acc[:])
 
         def transpose_and_quantise(x_sb, passes, codes, scales):
             x_words = x_sb[:].bitcast(F32)
@@ -266,31 +268,38 @@ def tile_fractalengine_pb_kernel(
         transpose_and_quantise(h_sb, HID_PASSES, h_codes, h_scales)
         transpose_and_quantise(eng_sb, 1, eng_codes, eng_scales)
 
-        for i in range(ROW_TILES):
-            prepare_plain_terms(0, i)
-        for gate, half in HALVES:
-            regroup(0, gate, half)
-            quantise(0, gate, half)
+        for gate in GATE_ORDER:
+            regroup(0, gate)
+            quantise(0, gate)
 
-        before = None
         for c in range(CHUNKS):
+            more = c + 1 < CHUNKS
+            if c + 2 < CHUNKS:
+                load_chunk(c + 2)
             for i in range(ROW_TILES):
-                ahead = HALVES[3 * i : 3 * i + 3] if c + 1 < CHUNKS else []
-                if i == 0 and c + 2 < CHUNKS:
-                    load_chunk(c + 2)
                 sigmoid_gate(c, i, R)
-                for gate, half in ahead:
-                    regroup(c + 1, gate, half)
-                if before is not None:
-                    blend(*before)
+            if more:
+                regroup(c + 1, R)
+            if c > 0:
+                for i in range(ROW_TILES):
+                    blend(c - 1, i)
+            for i in range(ROW_TILES):
+                hidden_part(c, i)
+            if more:
+                regroup(c + 1, N)
+            for i in range(ROW_TILES):
                 candidate(c, i)
-                for gate, half in ahead:
-                    quantise(c + 1, gate, half)
+            if more:
+                quantise(c + 1, R)
+                quantise(c + 1, N)
+                regroup(c + 1, Z)
+            if c > 0:
+                for i in range(ROW_TILES):
+                    mix_and_store(c - 1, i)
+            for i in range(ROW_TILES):
                 sigmoid_gate(c, i, Z)
-                if before is not None:
-                    mix_and_store(*before)
-                if c + 1 < CHUNKS:
-                    prepare_plain_terms(c + 1, i)
-                before = (c, i)
-        blend(*before)
-        mix_and_store(*before)
+            if more:
+                quantise(c + 1, Z)
+        for i in range(ROW_TILES):
+            blend(CHUNKS - 1, i)
+            mix_and_store(CHUNKS - 1, i)

@@ -111,10 +111,12 @@ def tile_fractalengine_pb_kernel(
                 grouped[c, gate, half] = stream.tile(
                     [P, CHUNK // 2, PACK], BF16, name="grouped", tag="grouped", bufs=6, align_bytes=64
                 )
-                nc.scalar.copy(
-                    out=grouped[c, gate, half][:].rearrange("p (c i) j -> p c j i", i=4),
-                    in_=raw[c, gate][:, :, half_cols(half)].rearrange("p j (c i) -> p c j i", i=4),
-                )
+                spread = grouped[c, gate, half][:].rearrange("p (c i) j -> p c j i", i=4)
+                runs = raw[c, gate][:, :, half_cols(half)].rearrange("p j (c i) -> p c j i", i=4)
+                if gate == Z and half == 1:
+                    nc.vector.tensor_copy(out=spread, in_=runs)
+                else:
+                    nc.scalar.copy(out=spread, in_=runs)
 
         def quantise(c, gate):
             wi_codes[c, gate] = stream.tile(
@@ -159,7 +161,7 @@ def tile_fractalengine_pb_kernel(
             )
 
         cand = {}
-        h_new = {}
+        step = {}
 
         def sigmoid_gate(c, i, gate):
             acc = bank([P, CHUNK], "acc")
@@ -184,17 +186,17 @@ def tile_fractalengine_pb_kernel(
             nc.vector.tensor_add(out=cand[c, i][:], in0=acc[:], in1=cand[c, i][:])
             nc.scalar.activation(out=cand[c, i][:], in_=cand[c, i][:], func=ACT.Tanh)
 
-        def blend(c, i):
-            h_new[c, i] = work.tile([P, CHUNK], F32, name="h_new", tag="h_new")
+        def step_to_old(c, i):
+            step[c, i] = work.tile([P, CHUNK], F32, name="step", tag="step")
             nc.vector.tensor_sub(
-                out=h_new[c, i][:], in0=h_sb[:, i, c * CHUNK : (c + 1) * CHUNK], in1=cand[c, i][:]
+                out=step[c, i][:], in0=h_sb[:, i, c * CHUNK : (c + 1) * CHUNK], in1=cand[c, i][:]
             )
-            nc.vector.tensor_mul(out=h_new[c, i][:], in0=h_new[c, i][:], in1=rz[:, Z, c, i, :])
-            nc.vector.tensor_add(out=h_new[c, i][:], in0=h_new[c, i][:], in1=cand[c, i][:])
+            nc.vector.tensor_mul(out=step[c, i][:], in0=step[c, i][:], in1=rz[:, Z, c, i, :])
 
         def mix_and_store(c, i):
             mixed = bank([P, CHUNK], "mix")
-            nc.tensor.matmul(out=mixed[:], lhsT=mix[:], rhs=h_new[c, i][:], start=True, stop=True)
+            nc.tensor.matmul(out=mixed[:], lhsT=mix[:], rhs=cand[c, i][:], start=True, stop=False)
+            nc.tensor.matmul(out=mixed[:], lhsT=mix[:], rhs=step[c, i][:], start=False, stop=True)
             result = work.tile([P, CHUNK], F32)
             nc.scalar.mul(out=result[:], in_=mixed[:], mul=0.05 / FACTION)
             nc.scalar.dma_start(out=out[row_tile(i), c * CHUNK : (c + 1) * CHUNK], in_=result[:])
@@ -282,7 +284,7 @@ def tile_fractalengine_pb_kernel(
                 regroup(c + 1, R)
             if c > 0:
                 for i in range(ROW_TILES):
-                    blend(c - 1, i)
+                    step_to_old(c - 1, i)
             for i in range(ROW_TILES):
                 hidden_part(c, i)
             if more:
@@ -301,5 +303,5 @@ def tile_fractalengine_pb_kernel(
             if more:
                 quantise(c + 1, Z)
         for i in range(ROW_TILES):
-            blend(CHUNKS - 1, i)
+            step_to_old(CHUNKS - 1, i)
             mix_and_store(CHUNKS - 1, i)

@@ -113,7 +113,7 @@ def tile_fractalengine_pb_kernel(
                 )
                 spread = grouped[c, gate, half][:].rearrange("p (c i) j -> p c j i", i=4)
                 runs = raw[c, gate][:, :, half_cols(half)].rearrange("p j (c i) -> p c j i", i=4)
-                if gate == Z and half == 1:
+                if c == 0:
                     nc.vector.tensor_copy(out=spread, in_=runs)
                 else:
                     nc.scalar.copy(out=spread, in_=runs)
@@ -161,7 +161,7 @@ def tile_fractalengine_pb_kernel(
             )
 
         cand = {}
-        step = {}
+        h_new = {}
 
         def sigmoid_gate(c, i, gate):
             acc = bank([P, CHUNK], "acc")
@@ -186,17 +186,17 @@ def tile_fractalengine_pb_kernel(
             nc.vector.tensor_add(out=cand[c, i][:], in0=acc[:], in1=cand[c, i][:])
             nc.scalar.activation(out=cand[c, i][:], in_=cand[c, i][:], func=ACT.Tanh)
 
-        def step_to_old(c, i):
-            step[c, i] = work.tile([P, CHUNK], F32, name="step", tag="step")
+        def blend(c, i):
+            h_new[c, i] = work.tile([P, CHUNK], F32, name="h_new", tag="h_new")
             nc.vector.tensor_sub(
-                out=step[c, i][:], in0=h_sb[:, i, c * CHUNK : (c + 1) * CHUNK], in1=cand[c, i][:]
+                out=h_new[c, i][:], in0=h_sb[:, i, c * CHUNK : (c + 1) * CHUNK], in1=cand[c, i][:]
             )
-            nc.vector.tensor_mul(out=step[c, i][:], in0=step[c, i][:], in1=rz[:, Z, c, i, :])
+            nc.vector.tensor_mul(out=h_new[c, i][:], in0=h_new[c, i][:], in1=rz[:, Z, c, i, :])
+            nc.vector.tensor_add(out=h_new[c, i][:], in0=h_new[c, i][:], in1=cand[c, i][:])
 
         def mix_and_store(c, i):
             mixed = bank([P, CHUNK], "mix")
-            nc.tensor.matmul(out=mixed[:], lhsT=mix[:], rhs=cand[c, i][:], start=True, stop=False)
-            nc.tensor.matmul(out=mixed[:], lhsT=mix[:], rhs=step[c, i][:], start=False, stop=True)
+            nc.tensor.matmul(out=mixed[:], lhsT=mix[:], rhs=h_new[c, i][:], start=True, stop=True)
             result = work.tile([P, CHUNK], F32)
             nc.scalar.mul(out=result[:], in_=mixed[:], mul=0.05 / FACTION)
             nc.scalar.dma_start(out=out[row_tile(i), c * CHUNK : (c + 1) * CHUNK], in_=result[:])
@@ -232,18 +232,6 @@ def tile_fractalengine_pb_kernel(
             out=mix[:], in0=ident[:], scalar=544.0, in1=mix[:], op0=ALU.mult, op1=ALU.add
         )
 
-        for c in range(CHUNKS):
-            for gate in (R, Z):
-                acc = bank([P, CHUNK], "acc")
-                plain_terms(acc, 0, c, gate)
-                nc.scalar.copy(out=rz[:, gate, c, 0, :], in_=acc[:])
-                acc = bank([P, CHUNK], "acc")
-                plain_terms(acc, 1, c, gate)
-                nc.vector.tensor_copy(out=rz[:, gate, c, 1, :], in_=acc[:])
-            acc = bank([P, CHUNK], "acc")
-            plain_terms(acc, ROW_TILES, c, N)
-            nc.scalar.copy(out=hid_bias[:, c, :], in_=acc[:])
-
         def transpose_and_quantise(x_sb, passes, codes, scales):
             x_words = x_sb[:].bitcast(F32)
             for g in range(passes):
@@ -258,9 +246,7 @@ def tile_fractalengine_pb_kernel(
                 x_grouped = stream.tile(
                     [P, CELLS, PACK], BF16, name="x_grouped", tag="grouped", bufs=6, align_bytes=64
                 )
-                nc.vector.tensor_copy(
-                    out=x_grouped[:].bitcast(F32), in_=flipped[:].rearrange("p u r -> p r u")
-                )
+                nc.scalar.copy(out=x_grouped[:].bitcast(F32), in_=flipped[:].rearrange("p u r -> p r u"))
                 nc.vector.quantize_mx(
                     out=codes[:, g, :].bitcast(FP8X4),
                     scales=scales[:, g, :],
@@ -269,6 +255,16 @@ def tile_fractalengine_pb_kernel(
 
         transpose_and_quantise(h_sb, HID_PASSES, h_codes, h_scales)
         transpose_and_quantise(eng_sb, 1, eng_codes, eng_scales)
+
+        for c in range(CHUNKS):
+            for gate in (R, Z):
+                for i in range(ROW_TILES):
+                    acc = bank([P, CHUNK], "acc")
+                    plain_terms(acc, i, c, gate)
+                    nc.scalar.copy(out=rz[:, gate, c, i, :], in_=acc[:])
+            acc = bank([P, CHUNK], "acc")
+            plain_terms(acc, ROW_TILES, c, N)
+            nc.scalar.copy(out=hid_bias[:, c, :], in_=acc[:])
 
         for gate in GATE_ORDER:
             regroup(0, gate)
@@ -281,27 +277,23 @@ def tile_fractalengine_pb_kernel(
             for i in range(ROW_TILES):
                 sigmoid_gate(c, i, R)
             if more:
-                regroup(c + 1, R)
+                for gate in GATE_ORDER:
+                    regroup(c + 1, gate)
             if c > 0:
                 for i in range(ROW_TILES):
-                    step_to_old(c - 1, i)
+                    blend(c - 1, i)
             for i in range(ROW_TILES):
                 hidden_part(c, i)
-            if more:
-                regroup(c + 1, N)
             for i in range(ROW_TILES):
                 candidate(c, i)
             if more:
-                quantise(c + 1, R)
-                quantise(c + 1, N)
-                regroup(c + 1, Z)
+                for gate in GATE_ORDER:
+                    quantise(c + 1, gate)
             if c > 0:
                 for i in range(ROW_TILES):
                     mix_and_store(c - 1, i)
             for i in range(ROW_TILES):
                 sigmoid_gate(c, i, Z)
-            if more:
-                quantise(c + 1, Z)
         for i in range(ROW_TILES):
-            step_to_old(CHUNKS - 1, i)
+            blend(CHUNKS - 1, i)
             mix_and_store(CHUNKS - 1, i)

@@ -31,6 +31,9 @@ FACTION = 32
 
 GATE_ORDER = (R, N, Z)
 
+WHOLE = slice(0, CHUNK)
+HALVES = (slice(0, CHUNK // 2), slice(CHUNK // 2, CHUNK))
+
 FLOPS = 2 * CELLS * GATES * D_HID * (D_IN + D_HID)
 
 
@@ -48,11 +51,12 @@ def tile_fractalengine_pb_kernel(
     with ExitStack() as ctx:
         keep = ctx.enter_context(tc.tile_pool(name="keep", bufs=1))
         stream = ctx.enter_context(tc.tile_pool(name="stream", bufs=1))
-        work = ctx.enter_context(tc.tile_pool(name="work", bufs=4))
+        work = ctx.enter_context(tc.tile_pool(name="work", bufs=2))
         psum = ctx.enter_context(tc.psum_pool(name="psum", bufs=1))
+        ctx.enter_context(tc.manual_schedule())
 
-        def bank(shape, tag):
-            return psum.tile(shape, F32, name=tag, tag=tag, bufs=6 if tag == "acc" else 2)
+        def bank(shape):
+            return psum.tile(shape, F32, name="acc", tag="acc", bufs=8)
 
         h_sb = keep.tile([P, ROW_TILES, D_HID], BF16)
         eng_sb = keep.tile([P, ROW_TILES, D_IN], BF16)
@@ -60,13 +64,16 @@ def tile_fractalengine_pb_kernel(
         h_scales = keep.tile([P, HID_PASSES, CELLS], U8, align_bytes=64)
         eng_codes = keep.tile([P, 1, CELLS], U32, align_bytes=64)
         eng_scales = keep.tile([P, 1, CELLS], U8, align_bytes=64)
-        wh_scales = keep.tile([P, HID_PASSES, GATES * D_HID], U8, align_bytes=64)
+        wh_scales = {}
+        for gate in GATE_ORDER:
+            for part, width in ((0, CHUNK), (1, D_HID - CHUNK)):
+                wh_scales[gate, part] = keep.tile(
+                    [P, HID_PASSES, width], U8, name="wh_scales_" + "rzn"[gate] + str(part), align_bytes=64
+                )
         ident = keep.tile([P, P], F32)
         mix = keep.tile([P, P], F32)
         left = keep.tile([P, ROW_TILES + 1, P], BF16)
         rows = keep.tile([P, GATES * D_HID], BF16)
-        rz = keep.tile([P, 2, CHUNKS, ROW_TILES, CHUNK], F32)
-        hid_bias = keep.tile([P, CHUNKS, CHUNK], F32)
 
         w_ih_packed = w_ih[0:D_IN, :].rearrange("(p j) n -> p j n", j=PACK)
         words_i32 = w_hh_words.bitcast(I32).rearrange("g p n -> p g n")
@@ -74,49 +81,42 @@ def tile_fractalengine_pb_kernel(
         raw = {}
         words = {}
 
-        def load_scale_rows(gate):
-            cols = slice(gate * D_HID, (gate + 1) * D_HID)
-            for half in range(2):
-                for r4 in range(4):
-                    q = 4 * half + r4
-                    nc.sync.dma_start(
-                        out=wh_scales[32 * half + r4 : P : 64, :, cols].bitcast(I32),
-                        in_=scales_i32[q : 16 : 8, :, gate * D_HID // 4 : (gate + 1) * D_HID // 4],
-                    )
-
-        def load_chunk(c):
-            for gate in GATE_ORDER:
-                raw[c, gate] = stream.tile([P, PACK, CHUNK], BF16, name="raw", tag="raw", bufs=6)
-                nc.sync.dma_start(out=raw[c, gate][:], in_=w_ih_packed[:, :, gate_cols(gate, c)])
-            for gate in GATE_ORDER:
-                if c == 0:
-                    load_scale_rows(gate)
-                words[c, gate] = stream.tile(
-                    [P, HID_PASSES, 2 * CHUNK], U8, name="words", tag="words", bufs=9, align_bytes=64
-                )
-                first = (gate * D_HID + c * CHUNK) // 2
+        def load_scale_rows(gate, part):
+            first = (gate * D_HID + part * CHUNK) // 4
+            last = (gate * D_HID + (D_HID if part else CHUNK)) // 4
+            for r4 in range(4):
                 nc.sync.dma_start(
-                    out=words[c, gate][:].bitcast(I32), in_=words_i32[:, :, first : first + CHUNK // 2]
+                    out=wh_scales[gate, part][r4 : P : 32, :, :].bitcast(I32),
+                    in_=scales_i32[r4 : 16 : 4, :, first:last],
                 )
+
+        def load_raw(c, gate):
+            raw[c, gate] = stream.tile([P, PACK, CHUNK], BF16, name="raw", tag="raw", bufs=8)
+            nc.sync.dma_start(out=raw[c, gate][:], in_=w_ih_packed[:, :, gate_cols(gate, c)])
+
+        def load_words(c, gate):
+            words[c, gate] = stream.tile(
+                [P, HID_PASSES, 2 * CHUNK], U8, name="words", tag="words", bufs=12, align_bytes=64
+            )
+            first = (gate * D_HID + c * CHUNK) // 2
+            nc.sync.dma_start(
+                out=words[c, gate][:].bitcast(I32), in_=words_i32[:, :, first : first + CHUNK // 2]
+            )
 
         grouped = {}
         wi_codes = {}
         wi_scales = {}
 
-        def half_cols(half):
-            return slice(half * CHUNK // 2, (half + 1) * CHUNK // 2)
-
-        def regroup(c, gate):
-            for half in range(2):
-                grouped[c, gate, half] = stream.tile(
-                    [P, CHUNK // 2, PACK], BF16, name="grouped", tag="grouped", bufs=6, align_bytes=64
+        def regroup(c, gate, half, engine_copy):
+            if half == 0:
+                grouped[c, gate] = stream.tile(
+                    [P, CHUNK, PACK], BF16, name="grouped", tag="grouped", bufs=4, align_bytes=64
                 )
-                spread = grouped[c, gate, half][:].rearrange("p (c i) j -> p c j i", i=4)
-                runs = raw[c, gate][:, :, half_cols(half)].rearrange("p j (c i) -> p c j i", i=4)
-                if c == 0:
-                    nc.vector.tensor_copy(out=spread, in_=runs)
-                else:
-                    nc.scalar.copy(out=spread, in_=runs)
+            cols = slice(half * CHUNK // 2, (half + 1) * CHUNK // 2)
+            engine_copy(
+                out=grouped[c, gate][:, cols, :].rearrange("p (c i) j -> p c j i", i=4),
+                in_=raw[c, gate][:, :, cols].rearrange("p j (c i) -> p c j i", i=4),
+            )
 
         def quantise(c, gate):
             wi_codes[c, gate] = stream.tile(
@@ -125,28 +125,32 @@ def tile_fractalengine_pb_kernel(
             wi_scales[c, gate] = stream.tile(
                 [P, CHUNK], U8, name="wi_scales", tag="wi_scales", bufs=6, align_bytes=64
             )
-            for half in range(2):
-                nc.vector.quantize_mx(
-                    out=wi_codes[c, gate][:, half_cols(half)].bitcast(FP8X4),
-                    scales=wi_scales[c, gate][:, half_cols(half)],
-                    in_=grouped[c, gate, half][:].rearrange("p w j -> p (w j)"),
-                )
+            nc.vector.quantize_mx(
+                out=wi_codes[c, gate][:].bitcast(FP8X4),
+                scales=wi_scales[c, gate][:],
+                in_=grouped[c, gate][:].rearrange("p w j -> p (w j)"),
+            )
 
-        def hidden_passes(acc, c, i, gate, stop):
+        acc = {}
+
+        def hidden_passes(c, i, gate, stop):
+            acc[c, i, gate] = bank([P, CHUNK])
             for g in range(HID_PASSES):
                 nc.tensor.matmul_mx(
-                    out=acc[:],
+                    out=acc[c, i, gate][:],
                     lhsT=h_codes[:, g, row_tile(i)].bitcast(FP8X4),
                     lhsT_scale=h_scales[:, g, row_tile(i)],
                     rhs=words[c, gate][:, g, :].bitcast(FP4X4),
-                    rhs_scale=wh_scales[:, g, gate_cols(gate, c)],
+                    rhs_scale=(
+                        wh_scales[gate, 1][:, g, (c - 1) * CHUNK : c * CHUNK] if c else wh_scales[gate, 0][:, g, :]
+                    ),
                     start=g == 0,
                     stop=stop and g == HID_PASSES - 1,
                 )
 
-        def input_pass(acc, c, i, gate, start):
+        def input_pass(to, c, i, gate, start):
             nc.tensor.matmul_mx(
-                out=acc[:],
+                out=to[:],
                 lhsT=eng_codes[:, 0, row_tile(i)].bitcast(FP8X4),
                 lhsT_scale=eng_scales[:, 0, row_tile(i)],
                 rhs=wi_codes[c, gate][:].bitcast(FP8X4),
@@ -155,75 +159,110 @@ def tile_fractalengine_pb_kernel(
                 stop=True,
             )
 
-        def plain_terms(acc, which, c, gate):
+        def plain_terms(which, c, gate):
+            to = bank([P, CHUNK])
             nc.tensor.matmul(
-                out=acc[:], lhsT=left[:, which, :], rhs=rows[:, gate_cols(gate, c)], start=True, stop=True
+                out=to[:], lhsT=left[:, which, :], rhs=rows[:, gate_cols(gate, c)], start=True, stop=True
             )
+            return to
 
+        sums = {}
+        hid_bias = {}
         cand = {}
         h_new = {}
 
-        def sigmoid_gate(c, i, gate):
-            acc = bank([P, CHUNK], "acc")
-            hidden_passes(acc, c, i, gate, stop=False)
-            input_pass(acc, c, i, gate, start=False)
-            nc.vector.tensor_add(out=rz[:, gate, c, i, :], in0=acc[:], in1=rz[:, gate, c, i, :])
-            nc.scalar.activation(out=rz[:, gate, c, i, :], in_=rz[:, gate, c, i, :], func=ACT.Sigmoid)
-
-        def hidden_part(c, i):
-            cand[c, i] = work.tile([P, CHUNK], F32, name="cand", tag="cand")
-            acc = bank([P, CHUNK], "acc")
-            hidden_passes(acc, c, i, N, stop=True)
-            nc.vector.tensor_add(out=cand[c, i][:], in0=acc[:], in1=hid_bias[:, c, :])
-
-        def candidate(c, i):
-            nc.vector.tensor_mul(out=cand[c, i][:], in0=cand[c, i][:], in1=rz[:, R, c, i, :])
-            acc = bank([P, CHUNK], "acc")
-            input_pass(acc, c, i, N, start=True)
-            nc.vector.tensor_add(out=cand[c, i][:], in0=acc[:], in1=cand[c, i][:])
-            acc = bank([P, CHUNK], "acc")
-            plain_terms(acc, i, c, N)
-            nc.vector.tensor_add(out=cand[c, i][:], in0=acc[:], in1=cand[c, i][:])
-            nc.scalar.activation(out=cand[c, i][:], in_=cand[c, i][:], func=ACT.Tanh)
-
-        def blend(c, i):
-            h_new[c, i] = work.tile([P, CHUNK], F32, name="h_new", tag="h_new")
-            nc.vector.tensor_sub(
-                out=h_new[c, i][:], in0=h_sb[:, i, c * CHUNK : (c + 1) * CHUNK], in1=cand[c, i][:]
+        def gate_terms(c, gate):
+            sums[c, gate] = work.tile(
+                [P, ROW_TILES, CHUNK], F32, name="sums_" + "rzn"[gate], tag="sums_" + "rzn"[gate]
             )
-            nc.vector.tensor_mul(out=h_new[c, i][:], in0=h_new[c, i][:], in1=rz[:, Z, c, i, :])
-            nc.vector.tensor_add(out=h_new[c, i][:], in0=h_new[c, i][:], in1=cand[c, i][:])
+            made = [plain_terms(i, c, gate) for i in range(ROW_TILES)]
+            for i in range(ROW_TILES):
+                nc.scalar.copy(out=sums[c, gate][:, i, :], in_=made[i][:])
 
-        def mix_and_store(c, i):
-            mixed = bank([P, CHUNK], "mix")
-            nc.tensor.matmul(out=mixed[:], lhsT=mix[:], rhs=h_new[c, i][:], start=True, stop=True)
-            result = work.tile([P, CHUNK], F32)
-            nc.scalar.mul(out=result[:], in_=mixed[:], mul=0.05 / FACTION)
-            nc.scalar.dma_start(out=out[row_tile(i), c * CHUNK : (c + 1) * CHUNK], in_=result[:])
+        def bias_term(c):
+            hid_bias[c] = work.tile([P, CHUNK], F32, name="hid_bias", tag="hid_bias")
+            terms = plain_terms(ROW_TILES, c, N)
+            nc.scalar.copy(out=hid_bias[c][:], in_=terms[:])
 
-        nc.vector.memset(rows[:].bitcast(I32), 0)
+        def gate_sum(c, i, gate):
+            nc.vector.tensor_add(
+                out=sums[c, gate][:, i, :], in0=acc[c, i, gate][:], in1=sums[c, gate][:, i, :]
+            )
+
+        def sigmoid(c, i, gate, cols):
+            part = sums[c, gate][:, i, cols]
+            nc.scalar.activation(out=part, in_=part, func=ACT.Sigmoid)
+
+        def hidden_part(c):
+            cand[c] = work.tile([P, ROW_TILES, CHUNK], F32, name="cand", tag="cand")
+            for i in range(ROW_TILES):
+                nc.vector.tensor_add(out=cand[c][:, i, :], in0=acc[c, i, N][:], in1=hid_bias[c][:])
+
+        def reset(c):
+            for i in range(ROW_TILES):
+                nc.vector.tensor_mul(
+                    out=cand[c][:, i, :], in0=cand[c][:, i, :], in1=sums[c, R][:, i, :]
+                )
+
+        given = {}
+        terms = {}
+
+        def candidate_matmuls(c):
+            for i in range(ROW_TILES):
+                given[c, i] = bank([P, CHUNK])
+                input_pass(given[c, i], c, i, N, start=True)
+            for i in range(ROW_TILES):
+                terms[c, i] = plain_terms(i, c, N)
+
+        def candidate(c):
+            for part in (given, terms):
+                for i in range(ROW_TILES):
+                    nc.vector.tensor_add(out=cand[c][:, i, :], in0=part[c, i][:], in1=cand[c][:, i, :])
+
+        def candidate_tanh(c):
+            for i in range(ROW_TILES):
+                nc.scalar.activation(out=cand[c][:, i, :], in_=cand[c][:, i, :], func=ACT.Tanh)
+
+        def blend_difference(c):
+            h_new[c] = work.tile([P, ROW_TILES, CHUNK], F32, name="h_new", tag="h_new")
+            nc.vector.tensor_sub(
+                out=h_new[c][:], in0=h_sb[:, :, c * CHUNK : (c + 1) * CHUNK], in1=cand[c][:]
+            )
+
+        def blend(c, pieces):
+            for i, cols in pieces:
+                part = h_new[c][:, i, cols]
+                nc.vector.tensor_mul(out=part, in0=part, in1=sums[c, Z][:, i, cols])
+            for i, cols in pieces:
+                part = h_new[c][:, i, cols]
+                nc.vector.tensor_add(out=part, in0=part, in1=cand[c][:, i, cols])
+
+        results = {}
+
+        def mix_factions(c, i, cols):
+            width = cols.stop - cols.start
+            mixed = bank([P, CHUNK])
+            nc.tensor.matmul(
+                out=mixed[:, 0:width], lhsT=mix[:], rhs=h_new[c][:, i, cols], start=True, stop=True
+            )
+            result = work.tile([P, CHUNK], F32, name="result", tag="result", bufs=6)
+            nc.scalar.mul(out=result[:, 0:width], in_=mixed[:, 0:width], mul=0.05 / FACTION)
+            nc.sync.dma_start(
+                out=out[row_tile(i), c * CHUNK + cols.start : c * CHUNK + cols.stop], in_=result[:, 0:width]
+            )
+
+        for i in range(ROW_TILES):
+            nc.sync.dma_start(out=h_sb[:, i, :], in_=hiddens[row_tile(i), :])
+        make_identity(nc, ident[:])
+        for gate in GATE_ORDER:
+            nc.gpsimd.memset(wh_scales[gate, 0][:].bitcast(I32), 0)
+        nc.gpsimd.memset(rows[:].bitcast(I32), 0)
+        for gate in GATE_ORDER:
+            nc.gpsimd.memset(wh_scales[gate, 1][:].bitcast(I32), 0)
         nc.vector.memset(left[:].bitcast(I32), 0)
         nc.vector.memset(left[32:33, 0:ROW_TILES, :], 1.0)
         nc.vector.memset(left[64:65, 0:ROW_TILES, :], 1.0)
         nc.vector.memset(left[96:97, ROW_TILES, :], 1.0)
-        nc.vector.memset(wh_scales[:].bitcast(I32), 0)
-        make_identity(nc, ident[:])
-
-        for i in range(ROW_TILES):
-            nc.sync.dma_start(out=h_sb[:, i, :], in_=hiddens[row_tile(i), :])
-        for i in range(ROW_TILES):
-            nc.sync.dma_start(out=eng_sb[:, i, :], in_=eng_out[row_tile(i), :])
-        nc.sync.dma_start(out=rows[0:1, :], in_=w_ih[D_IN : D_IN + 1, :])
-        nc.sync.dma_start(out=rows[32:33, :], in_=b_ih.rearrange("(o n) -> o n", o=1))
-        b_hh_row = b_hh.rearrange("(o n) -> o n", o=1)
-        nc.sync.dma_start(out=rows[64:65, 0 : N * D_HID], in_=b_hh_row[:, 0 : N * D_HID])
-        nc.sync.dma_start(out=rows[96:97, N * D_HID :], in_=b_hh_row[:, N * D_HID :])
-        nc.sync.dma_start(
-            out=left[0:1, 0:ROW_TILES, :], in_=tension.rearrange("(o i r) -> o i r", o=1, i=ROW_TILES)
-        )
-        load_chunk(0)
-        load_chunk(1)
-
         nc.vector.memset(mix[:], 0.0)
         for f in range(P // FACTION):
             block = slice(f * FACTION, (f + 1) * FACTION)
@@ -232,68 +271,123 @@ def tile_fractalengine_pb_kernel(
             out=mix[:], in0=ident[:], scalar=544.0, in1=mix[:], op0=ALU.mult, op1=ALU.add
         )
 
-        def transpose_and_quantise(x_sb, passes, codes, scales):
-            x_words = x_sb[:].bitcast(F32)
-            for g in range(passes):
-                flipped = bank([P, 2, CELLS], "acc")
-                for i in range(ROW_TILES):
-                    for u in range(2):
-                        nc.tensor.transpose(
-                            flipped[:, u, row_tile(i)],
-                            x_words[:, i, K_PASS // 2 * g + u : K_PASS // 2 * (g + 1) : 2],
-                            ident[:],
-                        )
-                x_grouped = stream.tile(
-                    [P, CELLS, PACK], BF16, name="x_grouped", tag="grouped", bufs=6, align_bytes=64
-                )
-                nc.scalar.copy(out=x_grouped[:].bitcast(F32), in_=flipped[:].rearrange("p u r -> p r u"))
-                nc.vector.quantize_mx(
-                    out=codes[:, g, :].bitcast(FP8X4),
-                    scales=scales[:, g, :],
-                    in_=x_grouped[:].rearrange("p r t -> p (r t)"),
-                )
-
-        transpose_and_quantise(h_sb, HID_PASSES, h_codes, h_scales)
-        transpose_and_quantise(eng_sb, 1, eng_codes, eng_scales)
-
-        for c in range(CHUNKS):
-            for gate in (R, Z):
-                for i in range(ROW_TILES):
-                    acc = bank([P, CHUNK], "acc")
-                    plain_terms(acc, i, c, gate)
-                    nc.scalar.copy(out=rz[:, gate, c, i, :], in_=acc[:])
-            acc = bank([P, CHUNK], "acc")
-            plain_terms(acc, ROW_TILES, c, N)
-            nc.scalar.copy(out=hid_bias[:, c, :], in_=acc[:])
-
+        b_hh_row = b_hh.rearrange("(o n) -> o n", o=1)
         for gate in GATE_ORDER:
-            regroup(0, gate)
-            quantise(0, gate)
+            load_words(0, gate)
+            load_scale_rows(gate, 0)
+            load_raw(0, gate)
+            if gate == GATE_ORDER[0]:
+                for i in range(ROW_TILES):
+                    nc.sync.dma_start(out=eng_sb[:, i, :], in_=eng_out[row_tile(i), :])
+                nc.sync.dma_start(out=rows[0:1, :], in_=w_ih[D_IN : D_IN + 1, :])
+                nc.sync.dma_start(out=rows[32:33, :], in_=b_ih.rearrange("(o n) -> o n", o=1))
+                nc.sync.dma_start(out=rows[64:65, 0 : N * D_HID], in_=b_hh_row[:, 0 : N * D_HID])
+                nc.sync.dma_start(out=rows[96:97, N * D_HID :], in_=b_hh_row[:, N * D_HID :])
+                nc.sync.dma_start(
+                    out=left[0:1, 0:ROW_TILES, :], in_=tension.rearrange("(o i r) -> o i r", o=1, i=ROW_TILES)
+                )
+
+        def load_chunk(c):
+            for gate in GATE_ORDER:
+                load_raw(c, gate)
+                if c == 1:
+                    load_scale_rows(gate, 1)
+                load_words(c, gate)
+
+        def transpose_and_quantise(x_sb, g, codes, scales):
+            x_words = x_sb[:].bitcast(F32)
+            flipped = bank([P, 2, CELLS])
+            for i in range(ROW_TILES):
+                for u in range(2):
+                    nc.tensor.transpose(
+                        flipped[:, u, row_tile(i)],
+                        x_words[:, i, K_PASS // 2 * g + u : K_PASS // 2 * (g + 1) : 2],
+                        ident[:],
+                    )
+            x_grouped = stream.tile([P, CELLS, PACK], BF16, name="x_grouped", tag="x_grouped", bufs=3, align_bytes=64)
+            nc.scalar.copy(out=x_grouped[:].bitcast(F32), in_=flipped[:].rearrange("p u r -> p r u"))
+            nc.vector.quantize_mx(
+                out=codes[:, g, :].bitcast(FP8X4),
+                scales=scales[:, g, :],
+                in_=x_grouped[:].rearrange("p r t -> p (r t)"),
+            )
+
+        for g in range(HID_PASSES):
+            transpose_and_quantise(h_sb, g, h_codes, h_scales)
+
+        both = range(ROW_TILES)
+
+        def regroup_gate(c, gate, engine_copy):
+            for half in range(2):
+                regroup(c, gate, half, engine_copy)
+
+        for i in both:
+            hidden_passes(0, i, R, stop=False)
+        transpose_and_quantise(eng_sb, 0, eng_codes, eng_scales)
+        bias_term(0)
+        gate_terms(0, R)
+        regroup_gate(0, R, nc.vector.tensor_copy)
+        quantise(0, R)
+        regroup_gate(0, N, nc.vector.tensor_copy)
+        quantise(0, N)
+        for c in range(1, CHUNKS):
+            load_chunk(c)
 
         for c in range(CHUNKS):
             more = c + 1 < CHUNKS
-            if c + 2 < CHUNKS:
-                load_chunk(c + 2)
-            for i in range(ROW_TILES):
-                sigmoid_gate(c, i, R)
-            if more:
-                for gate in GATE_ORDER:
-                    regroup(c + 1, gate)
             if c > 0:
-                for i in range(ROW_TILES):
-                    blend(c - 1, i)
-            for i in range(ROW_TILES):
-                hidden_part(c, i)
-            for i in range(ROW_TILES):
-                candidate(c, i)
-            if more:
-                for gate in GATE_ORDER:
-                    quantise(c + 1, gate)
+                for i in both:
+                    hidden_passes(c, i, R, stop=False)
+                blend(c - 1, [(i, WHOLE) for i in both])
+                regroup_gate(c, Z, nc.scalar.copy)
+            for i in both:
+                hidden_passes(c, i, N, stop=True)
+            if c > 0 and more:
+                regroup_gate(c + 1, R, nc.scalar.copy)
+            hidden_part(c)
+            for i in both:
+                input_pass(acc[c, i, R], c, i, R, start=False)
+            for i in both:
+                gate_sum(c, i, R)
+            for i in both:
+                sigmoid(c, i, R, WHOLE)
+            if c == 0:
+                gate_terms(0, Z)
+                gate_terms(1, R)
+                bias_term(1)
+            candidate_matmuls(c)
+            if c == 0:
+                regroup_gate(0, Z, nc.vector.tensor_copy)
+            quantise(c, Z)
             if c > 0:
-                for i in range(ROW_TILES):
-                    mix_and_store(c - 1, i)
-            for i in range(ROW_TILES):
-                sigmoid_gate(c, i, Z)
-        for i in range(ROW_TILES):
-            blend(CHUNKS - 1, i)
-            mix_and_store(CHUNKS - 1, i)
+                for i in both:
+                    mix_factions(c - 1, i, WHOLE)
+            reset(c)
+            if c > 0 and more:
+                gate_terms(c + 1, R)
+                bias_term(c + 1)
+            candidate(c)
+            candidate_tanh(c)
+            for i in both:
+                hidden_passes(c, i, Z, stop=False)
+                input_pass(acc[c, i, Z], c, i, Z, start=False)
+            if c == 0:
+                regroup_gate(1, R, nc.scalar.copy)
+            if more:
+                quantise(c + 1, R)
+            gate_sum(c, 0, Z)
+            blend_difference(c)
+            gate_sum(c, 1, Z)
+            if more:
+                regroup_gate(c + 1, N, nc.scalar.copy)
+            for i in both:
+                sigmoid(c, i, Z, WHOLE)
+            if more:
+                gate_terms(c + 1, Z)
+                quantise(c + 1, N)
+        last = CHUNKS - 1
+        for i in both:
+            blend(last, [(i, cols) for cols in HALVES])
+        for i in both:
+            for cols in HALVES:
+                mix_factions(last, i, cols)

@@ -254,15 +254,17 @@ def tile_fractalengine_pb_kernel(
         for i in range(ROW_TILES):
             nc.sync.dma_start(out=h_sb[:, i, :], in_=hiddens[row_tile(i), :])
         make_identity(nc, ident[:])
+        zero = keep.tile([P, 1], F32)
+        nc.vector.memset(zero[:], 0.0)
+        nc.scalar.copy(out=rows[:].bitcast(F32), in_=zero[:].to_broadcast([P, GATES * D_HID // 2]))
         for gate in GATE_ORDER:
-            nc.gpsimd.memset(wh_scales[gate, 0][:].bitcast(I32), 0)
-        nc.gpsimd.memset(rows[:].bitcast(I32), 0)
-        for gate in GATE_ORDER:
-            nc.gpsimd.memset(wh_scales[gate, 1][:].bitcast(I32), 0)
+            nc.vector.memset(wh_scales[gate, 0][:].bitcast(I32), 0)
         nc.vector.memset(left[:].bitcast(I32), 0)
         nc.vector.memset(left[32:33, 0:ROW_TILES, :], 1.0)
         nc.vector.memset(left[64:65, 0:ROW_TILES, :], 1.0)
         nc.vector.memset(left[96:97, ROW_TILES, :], 1.0)
+        for gate in GATE_ORDER:
+            nc.vector.memset(wh_scales[gate, 1][:].bitcast(I32), 0)
         nc.vector.memset(mix[:], 0.0)
         for f in range(P // FACTION):
             block = slice(f * FACTION, (f + 1) * FACTION)

@@ -66,9 +66,9 @@ def tile_fractalengine_pb_kernel(
         eng_scales = keep.tile([P, 1, CELLS], U8, align_bytes=64)
         wh_scales = {}
         for gate in GATE_ORDER:
-            for part, width in ((0, CHUNK), (1, D_HID - CHUNK)):
-                wh_scales[gate, part] = keep.tile(
-                    [P, HID_PASSES, width], U8, name="wh_scales_" + "rzn"[gate] + str(part), align_bytes=64
+            for c in range(CHUNKS):
+                wh_scales[gate, c] = keep.tile(
+                    [P, HID_PASSES, CHUNK], U8, name="wh_scales_" + "rzn"[gate] + str(c), align_bytes=64
                 )
         ident = keep.tile([P, P], F32)
         mix = keep.tile([P, P], F32)
@@ -81,12 +81,12 @@ def tile_fractalengine_pb_kernel(
         raw = {}
         words = {}
 
-        def load_scale_rows(gate, part):
-            first = (gate * D_HID + part * CHUNK) // 4
-            last = (gate * D_HID + (D_HID if part else CHUNK)) // 4
+        def load_scale_rows(gate, c):
+            first = (gate * D_HID + c * CHUNK) // 4
+            last = first + CHUNK // 4
             for r4 in range(4):
                 nc.sync.dma_start(
-                    out=wh_scales[gate, part][r4 : P : 32, :, :].bitcast(I32),
+                    out=wh_scales[gate, c][r4 : P : 32, :, :].bitcast(I32),
                     in_=scales_i32[r4 : 16 : 4, :, first:last],
                 )
 
@@ -141,9 +141,7 @@ def tile_fractalengine_pb_kernel(
                     lhsT=h_codes[:, g, row_tile(i)].bitcast(FP8X4),
                     lhsT_scale=h_scales[:, g, row_tile(i)],
                     rhs=words[c, gate][:, g, :].bitcast(FP4X4),
-                    rhs_scale=(
-                        wh_scales[gate, 1][:, g, (c - 1) * CHUNK : c * CHUNK] if c else wh_scales[gate, 0][:, g, :]
-                    ),
+                    rhs_scale=wh_scales[gate, c][:, g, :],
                     start=g == 0,
                     stop=stop and g == HID_PASSES - 1,
                 )
@@ -223,11 +221,12 @@ def tile_fractalengine_pb_kernel(
             for i in range(ROW_TILES):
                 nc.scalar.activation(out=cand[c][:, i, :], in_=cand[c][:, i, :], func=ACT.Tanh)
 
-        def blend_difference(c):
+        def blend_difference(c, engine):
             h_new[c] = work.tile([P, ROW_TILES, CHUNK], F32, name="h_new", tag="h_new")
-            nc.vector.tensor_sub(
-                out=h_new[c][:], in0=h_sb[:, :, c * CHUNK : (c + 1) * CHUNK], in1=cand[c][:]
-            )
+            for i in range(ROW_TILES):
+                engine.tensor_sub(
+                    out=h_new[c][:, i, :], in0=h_sb[:, i, c * CHUNK : (c + 1) * CHUNK], in1=cand[c][:, i, :]
+                )
 
         def blend(c, pieces):
             for i, cols in pieces:
@@ -239,20 +238,41 @@ def tile_fractalengine_pb_kernel(
 
         results = {}
 
-        def mix_factions(c, i, cols):
+        def blend_products(c, pieces):
+            for i, cols in pieces:
+                part = h_new[c][:, i, cols]
+                nc.vector.tensor_mul(out=part, in0=part, in1=sums[c, Z][:, i, cols])
+
+        mixed = {}
+
+        def mix_part(c, i, cols, part, start, stop):
             width = cols.stop - cols.start
-            mixed = bank([P, CHUNK])
+            if start:
+                mixed[c, i, cols.start] = bank([P, CHUNK])
             nc.tensor.matmul(
-                out=mixed[:, 0:width], lhsT=mix[:], rhs=h_new[c][:, i, cols], start=True, stop=True
+                out=mixed[c, i, cols.start][:, 0:width],
+                lhsT=mix[:],
+                rhs=part[c][:, i, cols],
+                start=start,
+                stop=stop,
             )
+
+        def scale_and_store(c, i, cols):
+            width = cols.stop - cols.start
             result = work.tile([P, CHUNK], F32, name="result", tag="result", bufs=6)
-            nc.scalar.mul(out=result[:, 0:width], in_=mixed[:, 0:width], mul=0.05 / FACTION)
+            nc.scalar.mul(out=result[:, 0:width], in_=mixed[c, i, cols.start][:, 0:width], mul=0.05 / FACTION)
             nc.sync.dma_start(
                 out=out[row_tile(i), c * CHUNK + cols.start : c * CHUNK + cols.stop], in_=result[:, 0:width]
             )
 
+        def mix_factions(c, i, cols):
+            mix_part(c, i, cols, h_new, start=True, stop=True)
+            scale_and_store(c, i, cols)
+
         for i in range(ROW_TILES):
             nc.sync.dma_start(out=h_sb[:, i, :], in_=hiddens[row_tile(i), :])
+        for i in range(ROW_TILES):
+            nc.sync.dma_start(out=eng_sb[:, i, :], in_=eng_out[row_tile(i), :])
         make_identity(nc, ident[:])
         zero = keep.tile([P, 1], F32)
         nc.vector.memset(zero[:], 0.0)
@@ -263,8 +283,9 @@ def tile_fractalengine_pb_kernel(
         nc.vector.memset(left[32:33, 0:ROW_TILES, :], 1.0)
         nc.vector.memset(left[64:65, 0:ROW_TILES, :], 1.0)
         nc.vector.memset(left[96:97, ROW_TILES, :], 1.0)
-        for gate in GATE_ORDER:
-            nc.vector.memset(wh_scales[gate, 1][:].bitcast(I32), 0)
+        for c in range(1, CHUNKS):
+            for gate in GATE_ORDER:
+                nc.vector.memset(wh_scales[gate, c][:].bitcast(I32), 0)
         nc.vector.memset(mix[:], 0.0)
         for f in range(P // FACTION):
             block = slice(f * FACTION, (f + 1) * FACTION)
@@ -279,8 +300,6 @@ def tile_fractalengine_pb_kernel(
             load_scale_rows(gate, 0)
             load_raw(0, gate)
             if gate == GATE_ORDER[0]:
-                for i in range(ROW_TILES):
-                    nc.sync.dma_start(out=eng_sb[:, i, :], in_=eng_out[row_tile(i), :])
                 nc.sync.dma_start(out=rows[0:1, :], in_=w_ih[D_IN : D_IN + 1, :])
                 nc.sync.dma_start(out=rows[32:33, :], in_=b_ih.rearrange("(o n) -> o n", o=1))
                 nc.sync.dma_start(out=rows[64:65, 0 : N * D_HID], in_=b_hh_row[:, 0 : N * D_HID])
@@ -292,8 +311,7 @@ def tile_fractalengine_pb_kernel(
         def load_chunk(c):
             for gate in GATE_ORDER:
                 load_raw(c, gate)
-                if c == 1:
-                    load_scale_rows(gate, 1)
+                load_scale_rows(gate, c)
                 load_words(c, gate)
 
         def transpose_and_quantise(x_sb, g, codes, scales):
@@ -318,22 +336,27 @@ def tile_fractalengine_pb_kernel(
             transpose_and_quantise(h_sb, g, h_codes, h_scales)
 
         both = range(ROW_TILES)
+        on_scalar = nc.scalar.copy
+        on_vector = nc.vector.tensor_copy
 
-        def regroup_gate(c, gate, engine_copy):
-            for half in range(2):
-                regroup(c, gate, half, engine_copy)
-
+        transpose_and_quantise(eng_sb, 0, eng_codes, eng_scales)
         for i in both:
             hidden_passes(0, i, R, stop=False)
-        transpose_and_quantise(eng_sb, 0, eng_codes, eng_scales)
         bias_term(0)
         gate_terms(0, R)
-        regroup_gate(0, R, nc.vector.tensor_copy)
+        for half in range(2):
+            regroup(0, R, half, on_vector)
         quantise(0, R)
-        regroup_gate(0, N, nc.vector.tensor_copy)
-        quantise(0, N)
         for c in range(1, CHUNKS):
             load_chunk(c)
+
+        def gate_r(c):
+            for i in both:
+                input_pass(acc[c, i, R], c, i, R, start=False)
+            for i in both:
+                gate_sum(c, i, R)
+            for i in both:
+                sigmoid(c, i, R, WHOLE)
 
         for c in range(CHUNKS):
             more = c + 1 < CHUNKS
@@ -341,55 +364,67 @@ def tile_fractalengine_pb_kernel(
                 for i in both:
                     hidden_passes(c, i, R, stop=False)
                 blend(c - 1, [(i, WHOLE) for i in both])
-                regroup_gate(c, Z, nc.scalar.copy)
-            for i in both:
-                hidden_passes(c, i, N, stop=True)
-            if c > 0 and more:
-                regroup_gate(c + 1, R, nc.scalar.copy)
-            hidden_part(c)
-            for i in both:
-                input_pass(acc[c, i, R], c, i, R, start=False)
-            for i in both:
-                gate_sum(c, i, R)
-            for i in both:
-                sigmoid(c, i, R, WHOLE)
+                regroup(c, Z, 0, on_scalar)
+                regroup(c, Z, 1, on_scalar)
             if c == 0:
+                gate_r(0)
                 gate_terms(0, Z)
                 gate_terms(1, R)
+            for i in both:
+                hidden_passes(c, i, N, stop=True)
+            if c == 0:
+                for half in range(2):
+                    regroup(0, N, half, on_vector)
+                quantise(0, N)
+            if c > 0 and more:
+                regroup(c + 1, R, 0, on_scalar)
+            hidden_part(c)
+            if c > 0:
+                gate_r(c)
+            if c > 0 and more:
+                regroup(c + 1, R, 1, on_scalar)
+            if c == 0:
                 bias_term(1)
             candidate_matmuls(c)
             if c == 0:
-                regroup_gate(0, Z, nc.vector.tensor_copy)
+                regroup(0, Z, 0, on_vector)
+                regroup(0, Z, 1, on_scalar)
+                for half in range(2):
+                    regroup(1, R, half, on_scalar)
             quantise(c, Z)
             if c > 0:
                 for i in both:
                     mix_factions(c - 1, i, WHOLE)
             reset(c)
             if c > 0 and more:
-                gate_terms(c + 1, R)
                 bias_term(c + 1)
             candidate(c)
+            if more:
+                regroup(c + 1, N, 0, on_vector)
             candidate_tanh(c)
             for i in both:
                 hidden_passes(c, i, Z, stop=False)
                 input_pass(acc[c, i, Z], c, i, Z, start=False)
-            if c == 0:
-                regroup_gate(1, R, nc.scalar.copy)
-            if more:
-                quantise(c + 1, R)
             gate_sum(c, 0, Z)
-            blend_difference(c)
+            blend_difference(c, nc.vector)
             gate_sum(c, 1, Z)
             if more:
-                regroup_gate(c + 1, N, nc.scalar.copy)
+                quantise(c + 1, R)
+                regroup(c + 1, N, 1, on_scalar)
             for i in both:
                 sigmoid(c, i, Z, WHOLE)
             if more:
+                if c > 0:
+                    gate_terms(c + 1, R)
                 gate_terms(c + 1, Z)
                 quantise(c + 1, N)
         last = CHUNKS - 1
         for i in both:
-            blend(last, [(i, cols) for cols in HALVES])
+            for cols in HALVES:
+                mix_part(last, i, cols, cand, start=True, stop=False)
+        for i in both:
+            blend_products(last, [(i, cols) for cols in HALVES])
         for i in both:
             for cols in HALVES:
-                mix_factions(last, i, cols)
+                mix_part(last, i, cols, h_new, start=False, stop=True)
+                scale_and_store(last, i, cols)

@@ -276,6 +276,8 @@ def tile_fractalengine_pb_kernel(
         make_identity(nc, ident[:])
         zero = keep.tile([P, 1], F32)
         nc.vector.memset(zero[:], 0.0)
+        warm = keep.tile([P, 1], F32)
+        nc.scalar.activation(out=warm[:], in_=zero[:], func=ACT.Sigmoid)
         nc.scalar.copy(out=rows[:].bitcast(F32), in_=zero[:].to_broadcast([P, GATES * D_HID // 2]))
         for gate in GATE_ORDER:
             nc.vector.memset(wh_scales[gate, 0][:].bitcast(I32), 0)
@@ -387,6 +389,7 @@ def tile_fractalengine_pb_kernel(
                 bias_term(1)
             candidate_matmuls(c)
             if c == 0:
+                reset(0)
                 regroup(0, Z, 0, on_vector)
                 regroup(0, Z, 1, on_scalar)
                 for half in range(2):
@@ -395,7 +398,7 @@ def tile_fractalengine_pb_kernel(
             if c > 0:
                 for i in both:
                     mix_factions(c - 1, i, WHOLE)
-            reset(c)
+                reset(c)
             if c > 0 and more:
                 bias_term(c + 1)
             candidate(c)

@@ -67,8 +67,12 @@ def tile_fractalengine_pb_kernel(
         wh_scales = {}
         for gate in GATE_ORDER:
             for c in range(CHUNKS):
-                wh_scales[gate, c] = keep.tile(
-                    [P, HID_PASSES, CHUNK], U8, name="wh_scales_" + "rzn"[gate] + str(c), align_bytes=64
+                wh_scales[gate, c] = (
+                    wh_scales[gate, c - 2]
+                    if c >= 2
+                    else keep.tile(
+                        [P, HID_PASSES, CHUNK], U8, name="wh_scales_" + "rzn"[gate] + str(c), align_bytes=64
+                    )
                 )
         ident = keep.tile([P, P], F32)
         mix = keep.tile([P, P], F32)
@@ -285,9 +289,8 @@ def tile_fractalengine_pb_kernel(
         nc.vector.memset(left[32:33, 0:ROW_TILES, :], 1.0)
         nc.vector.memset(left[64:65, 0:ROW_TILES, :], 1.0)
         nc.vector.memset(left[96:97, ROW_TILES, :], 1.0)
-        for c in range(1, CHUNKS):
-            for gate in GATE_ORDER:
-                nc.vector.memset(wh_scales[gate, c][:].bitcast(I32), 0)
+        for gate in GATE_ORDER:
+            nc.vector.memset(wh_scales[gate, 1][:].bitcast(I32), 0)
         nc.vector.memset(mix[:], 0.0)
         for f in range(P // FACTION):
             block = slice(f * FACTION, (f + 1) * FACTION)
@@ -298,9 +301,12 @@ def tile_fractalengine_pb_kernel(
 
         b_hh_row = b_hh.rearrange("(o n) -> o n", o=1)
         for gate in GATE_ORDER:
+            if gate != R:
+                load_raw(0, gate)
             load_words(0, gate)
             load_scale_rows(gate, 0)
-            load_raw(0, gate)
+            if gate == R:
+                load_raw(0, gate)
             if gate == GATE_ORDER[0]:
                 nc.sync.dma_start(out=rows[0:1, :], in_=w_ih[D_IN : D_IN + 1, :])
                 nc.sync.dma_start(out=rows[32:33, :], in_=b_ih.rearrange("(o n) -> o n", o=1))
@@ -344,13 +350,12 @@ def tile_fractalengine_pb_kernel(
         transpose_and_quantise(eng_sb, 0, eng_codes, eng_scales)
         for i in both:
             hidden_passes(0, i, R, stop=False)
-        bias_term(0)
         gate_terms(0, R)
+        bias_term(0)
         for half in range(2):
             regroup(0, R, half, on_vector)
         quantise(0, R)
-        for c in range(1, CHUNKS):
-            load_chunk(c)
+        load_chunk(1)
 
         def gate_r(c):
             for i in both:
@@ -360,8 +365,11 @@ def tile_fractalengine_pb_kernel(
             for i in both:
                 sigmoid(c, i, R, WHOLE)
 
+        last = CHUNKS - 1
         for c in range(CHUNKS):
             more = c + 1 < CHUNKS
+            if c > 0 and more:
+                load_chunk(c + 1)
             if c > 0:
                 for i in both:
                     hidden_passes(c, i, R, stop=False)
@@ -402,15 +410,20 @@ def tile_fractalengine_pb_kernel(
             if c > 0 and more:
                 bias_term(c + 1)
             candidate(c)
-            if more:
+            if 0 < c and more:
                 regroup(c + 1, N, 0, on_vector)
             candidate_tanh(c)
             for i in both:
                 hidden_passes(c, i, Z, stop=False)
                 input_pass(acc[c, i, Z], c, i, Z, start=False)
             gate_sum(c, 0, Z)
-            blend_difference(c, nc.vector)
+            if c == 0:
+                regroup(1, N, 0, on_scalar)
+            if c == last:
+                blend_difference(c, nc.vector)
             gate_sum(c, 1, Z)
+            if c < last:
+                blend_difference(c, nc.vector)
             if more:
                 quantise(c + 1, R)
                 regroup(c + 1, N, 1, on_scalar)
@@ -421,7 +434,6 @@ def tile_fractalengine_pb_kernel(
                     gate_terms(c + 1, R)
                 gate_terms(c + 1, Z)
                 quantise(c + 1, N)
-        last = CHUNKS - 1
         for i in both:
             for cols in HALVES:
                 mix_part(last, i, cols, cand, start=True, stop=False)

@@ -316,9 +316,13 @@ def tile_fractalengine_pb_kernel(
                     out=left[0:1, 0:ROW_TILES, :], in_=tension.rearrange("(o i r) -> o i r", o=1, i=ROW_TILES)
                 )
 
+        units = [(c, gate) for c in range(CHUNKS) for gate in GATE_ORDER]
+
         def load_chunk(c):
             for gate in GATE_ORDER:
-                load_raw(c, gate)
+                ahead = units.index((c, gate)) + 1
+                if ahead < len(units):
+                    load_raw(*units[ahead])
                 load_scale_rows(gate, c)
                 load_words(c, gate)
 
@@ -355,6 +359,7 @@ def tile_fractalengine_pb_kernel(
         for half in range(2):
             regroup(0, R, half, on_vector)
         quantise(0, R)
+        load_raw(1, R)
         load_chunk(1)
 
         def gate_r(c):
@@ -374,32 +379,30 @@ def tile_fractalengine_pb_kernel(
                 for i in both:
                     hidden_passes(c, i, R, stop=False)
                 blend(c - 1, [(i, WHOLE) for i in both])
-                regroup(c, Z, 0, on_scalar)
-                regroup(c, Z, 1, on_scalar)
+                for half in range(2):
+                    regroup(c, Z, half, on_scalar)
+            else:
+                regroup(0, N, 0, on_vector)
+            gate_r(c)
             if c == 0:
-                gate_r(0)
                 gate_terms(0, Z)
                 gate_terms(1, R)
             for i in both:
                 hidden_passes(c, i, N, stop=True)
             if c == 0:
-                for half in range(2):
-                    regroup(0, N, half, on_vector)
+                regroup(0, N, 1, on_vector)
                 quantise(0, N)
-            if c > 0 and more:
+                regroup(0, Z, 0, on_vector)
+            elif more:
                 regroup(c + 1, R, 0, on_scalar)
             hidden_part(c)
-            if c > 0:
-                gate_r(c)
             if c > 0 and more:
                 regroup(c + 1, R, 1, on_scalar)
-            if c == 0:
-                bias_term(1)
             candidate_matmuls(c)
             if c == 0:
                 reset(0)
-                regroup(0, Z, 0, on_vector)
                 regroup(0, Z, 1, on_scalar)
+                bias_term(1)
                 for half in range(2):
                     regroup(1, R, half, on_scalar)
             quantise(c, Z)
@@ -407,10 +410,10 @@ def tile_fractalengine_pb_kernel(
                 for i in both:
                     mix_factions(c - 1, i, WHOLE)
                 reset(c)
-            if c > 0 and more:
-                bias_term(c + 1)
+                if more:
+                    bias_term(c + 1)
             candidate(c)
-            if 0 < c and more:
+            if c > 0 and more:
                 regroup(c + 1, N, 0, on_vector)
             candidate_tanh(c)
             for i in both:
@@ -422,11 +425,13 @@ def tile_fractalengine_pb_kernel(
             if c == last:
                 blend_difference(c, nc.vector)
             gate_sum(c, 1, Z)
-            if c < last:
-                blend_difference(c, nc.vector)
             if more:
                 quantise(c + 1, R)
-                regroup(c + 1, N, 1, on_scalar)
+                if c == 0:
+                    regroup(1, N, 1, on_vector)
+                else:
+                    regroup(c + 1, N, 1, on_scalar)
+                blend_difference(c, nc.vector)
             for i in both:
                 sigmoid(c, i, Z, WHOLE)
             if more:

@@ -76,8 +76,11 @@ def tile_fractalengine_pb_kernel(
                 )
         ident = keep.tile([P, P], F32)
         mix = keep.tile([P, P], F32)
+        mix_parts = keep.tile([P, 2, P], BF16)
         left = keep.tile([P, ROW_TILES + 1, P], BF16)
-        rows = keep.tile([P, GATES * D_HID], BF16)
+        rows = [
+            keep.tile([P, GATES, D_HID // 2], BF16, name="rows_" + str(half)) for half in range(2)
+        ]
 
         w_ih_packed = w_ih[0:D_IN, :].rearrange("(p j) n -> p j n", j=PACK)
         words_i32 = w_hh_words.bitcast(I32).rearrange("g p n -> p g n")
@@ -164,7 +167,7 @@ def tile_fractalengine_pb_kernel(
         def plain_terms(which, c, gate):
             to = bank([P, CHUNK])
             nc.tensor.matmul(
-                out=to[:], lhsT=left[:, which, :], rhs=rows[:, gate_cols(gate, c)], start=True, stop=True
+                out=to[:], lhsT=left[:, which, :], rhs=rows[c // 2][:, gate, c % 2 * CHUNK : (c % 2 + 1) * CHUNK], start=True, stop=True
             )
             return to
 
@@ -225,12 +228,12 @@ def tile_fractalengine_pb_kernel(
             for i in range(ROW_TILES):
                 nc.scalar.activation(out=cand[c][:, i, :], in_=cand[c][:, i, :], func=ACT.Tanh)
 
-        def blend_difference(c, engine):
-            h_new[c] = work.tile([P, ROW_TILES, CHUNK], F32, name="h_new", tag="h_new")
-            for i in range(ROW_TILES):
-                engine.tensor_sub(
-                    out=h_new[c][:, i, :], in0=h_sb[:, i, c * CHUNK : (c + 1) * CHUNK], in1=cand[c][:, i, :]
-                )
+        def blend_difference(c, i):
+            if i == 0:
+                h_new[c] = work.tile([P, ROW_TILES, CHUNK], F32, name="h_new", tag="h_new")
+            nc.vector.tensor_sub(
+                out=h_new[c][:, i, :], in0=h_sb[:, i, c * CHUNK : (c + 1) * CHUNK], in1=cand[c][:, i, :]
+            )
 
         def blend(c, pieces):
             for i, cols in pieces:
@@ -242,23 +245,37 @@ def tile_fractalengine_pb_kernel(
 
         results = {}
 
-        def blend_products(c, pieces):
+        def pull(c, pieces):
             for i, cols in pieces:
                 part = h_new[c][:, i, cols]
-                nc.vector.tensor_mul(out=part, in0=part, in1=sums[c, Z][:, i, cols])
+                nc.vector.scalar_tensor_tensor(
+                    out=part, in0=sums[c, Z][:, i, cols], scalar=-1.0, in1=part, op0=ALU.add, op1=ALU.mult
+                )
 
         mixed = {}
 
-        def mix_part(c, i, cols, part, start, stop):
+        def mix_hiddens(c, i, cols):
+            width = cols.stop - cols.start
+            mixed[c, i, cols.start] = bank([P, CHUNK])
+            for part in range(2):
+                nc.tensor.matmul(
+                    out=mixed[c, i, cols.start][:, 0:width],
+                    lhsT=mix_parts[:, part, :],
+                    rhs=h_sb[:, i, c * CHUNK + cols.start : c * CHUNK + cols.stop],
+                    start=part == 0,
+                    stop=False,
+                )
+
+        def mix_part(c, i, cols, start):
             width = cols.stop - cols.start
             if start:
                 mixed[c, i, cols.start] = bank([P, CHUNK])
             nc.tensor.matmul(
                 out=mixed[c, i, cols.start][:, 0:width],
                 lhsT=mix[:],
-                rhs=part[c][:, i, cols],
+                rhs=h_new[c][:, i, cols],
                 start=start,
-                stop=stop,
+                stop=True,
             )
 
         def scale_and_store(c, i, cols):
@@ -270,7 +287,7 @@ def tile_fractalengine_pb_kernel(
             )
 
         def mix_factions(c, i, cols):
-            mix_part(c, i, cols, h_new, start=True, stop=True)
+            mix_part(c, i, cols, start=True)
             scale_and_store(c, i, cols)
 
         for i in range(ROW_TILES):
@@ -282,7 +299,11 @@ def tile_fractalengine_pb_kernel(
         nc.vector.memset(zero[:], 0.0)
         warm = keep.tile([P, 1], F32)
         nc.scalar.activation(out=warm[:], in_=zero[:], func=ACT.Sigmoid)
-        nc.scalar.copy(out=rows[:].bitcast(F32), in_=zero[:].to_broadcast([P, GATES * D_HID // 2]))
+        for half in range(2):
+            nc.scalar.copy(
+                out=rows[half][:].rearrange("p g n -> p (g n)").bitcast(F32),
+                in_=zero[:].to_broadcast([P, GATES * D_HID // 4]),
+            )
         for gate in GATE_ORDER:
             nc.vector.memset(wh_scales[gate, 0][:].bitcast(I32), 0)
         nc.vector.memset(left[:].bitcast(I32), 0)
@@ -295,11 +316,22 @@ def tile_fractalengine_pb_kernel(
         for f in range(P // FACTION):
             block = slice(f * FACTION, (f + 1) * FACTION)
             nc.vector.memset(mix[block, block], 3.0)
+        nc.vector.tensor_scalar_mul(out=mix_parts[:, 0, :], in0=ident[:], scalar1=544.0)
+        nc.vector.tensor_copy(out=mix_parts[:, 1, :], in_=mix[:])
         nc.vector.scalar_tensor_tensor(
             out=mix[:], in0=ident[:], scalar=544.0, in1=mix[:], op0=ALU.mult, op1=ALU.add
         )
 
-        b_hh_row = b_hh.rearrange("(o n) -> o n", o=1)
+        def load_rows(half):
+            cols = slice(half * D_HID // 2, (half + 1) * D_HID // 2)
+            w_row = w_ih[D_IN : D_IN + 1, :].rearrange("o (g n) -> o g n", g=GATES)
+            b_ih_row = b_ih.rearrange("(o g n) -> o g n", o=1, g=GATES)
+            b_hh_row = b_hh.rearrange("(o g n) -> o g n", o=1, g=GATES)
+            nc.sync.dma_start(out=rows[half][0:1, :, :], in_=w_row[:, :, cols])
+            nc.sync.dma_start(out=rows[half][32:33, :, :], in_=b_ih_row[:, :, cols])
+            nc.sync.dma_start(out=rows[half][64:65, 0:N, :], in_=b_hh_row[:, 0:N, cols])
+            nc.sync.dma_start(out=rows[half][96:97, N:GATES, :], in_=b_hh_row[:, N:GATES, cols])
+
         for gate in GATE_ORDER:
             if gate != R:
                 load_raw(0, gate)
@@ -308,10 +340,7 @@ def tile_fractalengine_pb_kernel(
             if gate == R:
                 load_raw(0, gate)
             if gate == GATE_ORDER[0]:
-                nc.sync.dma_start(out=rows[0:1, :], in_=w_ih[D_IN : D_IN + 1, :])
-                nc.sync.dma_start(out=rows[32:33, :], in_=b_ih.rearrange("(o n) -> o n", o=1))
-                nc.sync.dma_start(out=rows[64:65, 0 : N * D_HID], in_=b_hh_row[:, 0 : N * D_HID])
-                nc.sync.dma_start(out=rows[96:97, N * D_HID :], in_=b_hh_row[:, N * D_HID :])
+                load_rows(0)
                 nc.sync.dma_start(
                     out=left[0:1, 0:ROW_TILES, :], in_=tension.rearrange("(o i r) -> o i r", o=1, i=ROW_TILES)
                 )
@@ -325,6 +354,8 @@ def tile_fractalengine_pb_kernel(
                     load_raw(*units[ahead])
                 load_scale_rows(gate, c)
                 load_words(c, gate)
+                if (c, gate) == (1, Z):
+                    load_rows(1)
 
         def transpose_and_quantise(x_sb, g, codes, scales):
             x_words = x_sb[:].bitcast(F32)
@@ -414,6 +445,7 @@ def tile_fractalengine_pb_kernel(
                     bias_term(c + 1)
             candidate(c)
             if c > 0 and more:
+                quantise(c + 1, R)
                 regroup(c + 1, N, 0, on_vector)
             candidate_tanh(c)
             for i in both:
@@ -423,15 +455,16 @@ def tile_fractalengine_pb_kernel(
             if c == 0:
                 regroup(1, N, 0, on_scalar)
             if c == last:
-                blend_difference(c, nc.vector)
+                blend_difference(c, 0)
             gate_sum(c, 1, Z)
             if more:
-                quantise(c + 1, R)
                 if c == 0:
+                    quantise(1, R)
                     regroup(1, N, 1, on_vector)
                 else:
                     regroup(c + 1, N, 1, on_scalar)
-                blend_difference(c, nc.vector)
+                for i in both:
+                    blend_difference(c, i)
             for i in both:
                 sigmoid(c, i, Z, WHOLE)
             if more:
@@ -441,10 +474,11 @@ def tile_fractalengine_pb_kernel(
                 quantise(c + 1, N)
         for i in both:
             for cols in HALVES:
-                mix_part(last, i, cols, cand, start=True, stop=False)
-        for i in both:
-            blend_products(last, [(i, cols) for cols in HALVES])
+                mix_hiddens(last, i, cols)
+        pull(last, [(0, cols) for cols in HALVES])
+        blend_difference(last, 1)
+        pull(last, [(1, cols) for cols in HALVES])
         for i in both:
             for cols in HALVES:
-                mix_part(last, i, cols, h_new, start=False, stop=True)
+                mix_part(last, i, cols, start=False)
                 scale_and_store(last, i, cols)

from contextlib import ExitStack

import concourse.mybir as mybir
from concourse.masks import make_identity

F32 = mybir.dt.float32
BF16 = mybir.dt.bfloat16
I32 = mybir.dt.int32
U32 = mybir.dt.uint32
U8 = mybir.dt.uint8
FP8X4 = mybir.dt.float8_e4m3fn_x4
FP4X4 = mybir.dt.float4_e2m1fn_x4
ALU = mybir.AluOpType
ACT = mybir.ActivationFunctionType

P = 128
PACK = 4
K_PASS = P * PACK
CELLS = 256
ROW_TILES = CELLS // P
D_IN = 512
D_HID = 2048
HID_PASSES = D_HID // K_PASS
GATES = 3
R = 0
Z = 1
N = 2
CHUNK = 512
CHUNKS = D_HID // CHUNK
FACTION = 32

GATE_ORDER = (R, N, Z)

WHOLE = slice(0, CHUNK)
HALVES = (slice(0, CHUNK // 2), slice(CHUNK // 2, CHUNK))

FLOPS = 2 * CELLS * GATES * D_HID * (D_IN + D_HID)


def tile_fractalengine_pb_kernel(
    tc, eng_out, tension, hiddens, w_ih, b_ih, w_hh_words, w_hh_scales, b_hh, out
):
    nc = tc.nc

    def gate_cols(gate, c):
        return slice(gate * D_HID + c * CHUNK, gate * D_HID + (c + 1) * CHUNK)

    def row_tile(i):
        return slice(i * P, (i + 1) * P)

    with ExitStack() as ctx:
        keep = ctx.enter_context(tc.tile_pool(name="keep", bufs=1))
        stream = ctx.enter_context(tc.tile_pool(name="stream", bufs=1))
        work = ctx.enter_context(tc.tile_pool(name="work", bufs=2))
        psum = ctx.enter_context(tc.psum_pool(name="psum", bufs=1))
        ctx.enter_context(tc.manual_schedule())

        def bank(shape):
            return psum.tile(shape, F32, name="acc", tag="acc", bufs=8)

        h_sb = keep.tile([P, ROW_TILES, D_HID], BF16)
        eng_sb = keep.tile([P, ROW_TILES, D_IN], BF16)
        h_codes = keep.tile([P, HID_PASSES, CELLS], U32, align_bytes=64)
        h_scales = keep.tile([P, HID_PASSES, CELLS], U8, align_bytes=64)
        eng_codes = keep.tile([P, 1, CELLS], U32, align_bytes=64)
        eng_scales = keep.tile([P, 1, CELLS], U8, align_bytes=64)
        wh_scales = {}
        for gate in GATE_ORDER:
            for c in range(CHUNKS):
                wh_scales[gate, c] = (
                    wh_scales[gate, c - 2]
                    if c >= 2
                    else keep.tile(
                        [P, HID_PASSES, CHUNK], U8, name="wh_scales_" + "rzn"[gate] + str(c), align_bytes=64
                    )
                )
        ident = keep.tile([P, P], F32)
        mix = keep.tile([P, P], F32)
        mix_parts = keep.tile([P, 2, P], BF16)
        left = keep.tile([P, ROW_TILES + 1, P], BF16)
        rows = [
            keep.tile([P, GATES, D_HID // 2], BF16, name="rows_" + str(half)) for half in range(2)
        ]

        w_ih_packed = w_ih[0:D_IN, :].rearrange("(p j) n -> p j n", j=PACK)
        words_i32 = w_hh_words.bitcast(I32).rearrange("g p n -> p g n")
        scales_i32 = w_hh_scales.bitcast(I32).rearrange("g q n -> q g n")
        raw = {}
        words = {}

        def load_scale_rows(gate, c):
            first = (gate * D_HID + c * CHUNK) // 4
            last = first + CHUNK // 4
            for r4 in range(4):
                nc.sync.dma_start(
                    out=wh_scales[gate, c][r4 : P : 32, :, :].bitcast(I32),
                    in_=scales_i32[r4 : 16 : 4, :, first:last],
                )

        def load_raw(c, gate):
            raw[c, gate] = stream.tile([P, PACK, CHUNK], BF16, name="raw", tag="raw", bufs=8)
            nc.sync.dma_start(out=raw[c, gate][:], in_=w_ih_packed[:, :, gate_cols(gate, c)])

        def load_words(c, gate):
            words[c, gate] = stream.tile(
                [P, HID_PASSES, 2 * CHUNK], U8, name="words", tag="words", bufs=12, align_bytes=64
            )
            first = (gate * D_HID + c * CHUNK) // 2
            nc.sync.dma_start(
                out=words[c, gate][:].bitcast(I32), in_=words_i32[:, :, first : first + CHUNK // 2]
            )

        grouped = {}
        wi_codes = {}
        wi_scales = {}

        def regroup(c, gate, half, engine_copy):
            if half == 0:
                grouped[c, gate] = stream.tile(
                    [P, CHUNK, PACK], BF16, name="grouped", tag="grouped", bufs=4, align_bytes=64
                )
            cols = slice(half * CHUNK // 2, (half + 1) * CHUNK // 2)
            engine_copy(
                out=grouped[c, gate][:, cols, :].rearrange("p (c i) j -> p c j i", i=4),
                in_=raw[c, gate][:, :, cols].rearrange("p j (c i) -> p c j i", i=4),
            )

        def quantise(c, gate):
            wi_codes[c, gate] = stream.tile(
                [P, CHUNK], U32, name="wi_codes", tag="wi_codes", bufs=6, align_bytes=64
            )
            wi_scales[c, gate] = stream.tile(
                [P, CHUNK], U8, name="wi_scales", tag="wi_scales", bufs=6, align_bytes=64
            )
            nc.vector.quantize_mx(
                out=wi_codes[c, gate][:].bitcast(FP8X4),
                scales=wi_scales[c, gate][:],
                in_=grouped[c, gate][:].rearrange("p w j -> p (w j)"),
            )

        acc = {}

        def hidden_passes(c, i, gate, stop):
            acc[c, i, gate] = bank([P, CHUNK])
            for g in range(HID_PASSES):
                nc.tensor.matmul_mx(
                    out=acc[c, i, gate][:],
                    lhsT=h_codes[:, g, row_tile(i)].bitcast(FP8X4),
                    lhsT_scale=h_scales[:, g, row_tile(i)],
                    rhs=words[c, gate][:, g, :].bitcast(FP4X4),
                    rhs_scale=wh_scales[gate, c][:, g, :],
                    start=g == 0,
                    stop=stop and g == HID_PASSES - 1,
                )

        def input_pass(to, c, i, gate, start):
            nc.tensor.matmul_mx(
                out=to[:],
                lhsT=eng_codes[:, 0, row_tile(i)].bitcast(FP8X4),
                lhsT_scale=eng_scales[:, 0, row_tile(i)],
                rhs=wi_codes[c, gate][:].bitcast(FP8X4),
                rhs_scale=wi_scales[c, gate][:],
                start=start,
                stop=True,
            )

        def plain_terms(which, c, gate):
            to = bank([P, CHUNK])
            nc.tensor.matmul(
                out=to[:], lhsT=left[:, which, :], rhs=rows[c // 2][:, gate, c % 2 * CHUNK : (c % 2 + 1) * CHUNK], start=True, stop=True
            )
            return to

        sums = {}
        hid_bias = {}
        cand = {}
        h_new = {}

        def gate_terms(c, gate):
            sums[c, gate] = work.tile(
                [P, ROW_TILES, CHUNK], F32, name="sums_" + "rzn"[gate], tag="sums_" + "rzn"[gate]
            )
            made = [plain_terms(i, c, gate) for i in range(ROW_TILES)]
            for i in range(ROW_TILES):
                nc.scalar.copy(out=sums[c, gate][:, i, :], in_=made[i][:])

        def bias_term(c):
            hid_bias[c] = work.tile([P, CHUNK], F32, name="hid_bias", tag="hid_bias")
            terms = plain_terms(ROW_TILES, c, N)
            nc.scalar.copy(out=hid_bias[c][:], in_=terms[:])

        def gate_sum(c, i, gate):
            nc.vector.tensor_add(
                out=sums[c, gate][:, i, :], in0=acc[c, i, gate][:], in1=sums[c, gate][:, i, :]
            )

        def sigmoid(c, i, gate, cols):
            part = sums[c, gate][:, i, cols]
            nc.scalar.activation(out=part, in_=part, func=ACT.Sigmoid)

        def hidden_part(c):
            cand[c] = work.tile([P, ROW_TILES, CHUNK], F32, name="cand", tag="cand")
            for i in range(ROW_TILES):
                nc.vector.tensor_add(out=cand[c][:, i, :], in0=acc[c, i, N][:], in1=hid_bias[c][:])

        def reset(c):
            for i in range(ROW_TILES):
                nc.vector.tensor_mul(
                    out=cand[c][:, i, :], in0=cand[c][:, i, :], in1=sums[c, R][:, i, :]
                )

        given = {}
        terms = {}

        def candidate_matmuls(c):
            for i in range(ROW_TILES):
                given[c, i] = bank([P, CHUNK])
                input_pass(given[c, i], c, i, N, start=True)
            for i in range(ROW_TILES):
                terms[c, i] = plain_terms(i, c, N)

        def candidate(c):
            for part in (given, terms):
                for i in range(ROW_TILES):
                    nc.vector.tensor_add(out=cand[c][:, i, :], in0=part[c, i][:], in1=cand[c][:, i, :])

        def candidate_tanh(c):
            for i in range(ROW_TILES):
                nc.scalar.activation(out=cand[c][:, i, :], in_=cand[c][:, i, :], func=ACT.Tanh)

        def blend_difference(c, i):
            if i == 0:
                h_new[c] = work.tile([P, ROW_TILES, CHUNK], F32, name="h_new", tag="h_new")
            nc.vector.tensor_sub(
                out=h_new[c][:, i, :], in0=h_sb[:, i, c * CHUNK : (c + 1) * CHUNK], in1=cand[c][:, i, :]
            )

        def blend(c, pieces):
            for i, cols in pieces:
                part = h_new[c][:, i, cols]
                nc.vector.tensor_mul(out=part, in0=part, in1=sums[c, Z][:, i, cols])
            for i, cols in pieces:
                part = h_new[c][:, i, cols]
                nc.vector.tensor_add(out=part, in0=part, in1=cand[c][:, i, cols])

        results = {}

        def pull(c, pieces):
            for i, cols in pieces:
                part = h_new[c][:, i, cols]
                nc.vector.scalar_tensor_tensor(
                    out=part, in0=sums[c, Z][:, i, cols], scalar=-1.0, in1=part, op0=ALU.add, op1=ALU.mult
                )

        mixed = {}

        def mix_hiddens(c, i, cols):
            width = cols.stop - cols.start
            mixed[c, i, cols.start] = bank([P, CHUNK])
            for part in range(2):
                nc.tensor.matmul(
                    out=mixed[c, i, cols.start][:, 0:width],
                    lhsT=mix_parts[:, part, :],
                    rhs=h_sb[:, i, c * CHUNK + cols.start : c * CHUNK + cols.stop],
                    start=part == 0,
                    stop=False,
                )

        def mix_part(c, i, cols, start):
            width = cols.stop - cols.start
            if start:
                mixed[c, i, cols.start] = bank([P, CHUNK])
            nc.tensor.matmul(
                out=mixed[c, i, cols.start][:, 0:width],
                lhsT=mix[:],
                rhs=h_new[c][:, i, cols],
                start=start,
                stop=True,
            )

        def scale_and_store(c, i, cols):
            width = cols.stop - cols.start
            result = work.tile([P, CHUNK], F32, name="result", tag="result", bufs=6)
            nc.scalar.mul(out=result[:, 0:width], in_=mixed[c, i, cols.start][:, 0:width], mul=0.05 / FACTION)
            nc.sync.dma_start(
                out=out[row_tile(i), c * CHUNK + cols.start : c * CHUNK + cols.stop], in_=result[:, 0:width]
            )

        def mix_factions(c, i, cols):
            mix_part(c, i, cols, start=True)
            scale_and_store(c, i, cols)

        for i in range(ROW_TILES):
            nc.sync.dma_start(out=h_sb[:, i, :], in_=hiddens[row_tile(i), :])
        for i in range(ROW_TILES):
            nc.sync.dma_start(out=eng_sb[:, i, :], in_=eng_out[row_tile(i), :])
        make_identity(nc, ident[:])
        zero = keep.tile([P, 1], F32)
        nc.vector.memset(zero[:], 0.0)
        warm = keep.tile([P, 1], F32)
        nc.scalar.activation(out=warm[:], in_=zero[:], func=ACT.Sigmoid)
        for half in range(2):
            nc.scalar.copy(
                out=rows[half][:].rearrange("p g n -> p (g n)").bitcast(F32),
                in_=zero[:].to_broadcast([P, GATES * D_HID // 4]),
            )
        for gate in GATE_ORDER:
            nc.vector.memset(wh_scales[gate, 0][:].bitcast(I32), 0)
        nc.vector.memset(left[:].bitcast(I32), 0)
        nc.vector.memset(left[32:33, 0:ROW_TILES, :], 1.0)
        nc.vector.memset(left[64:65, 0:ROW_TILES, :], 1.0)
        nc.vector.memset(left[96:97, ROW_TILES, :], 1.0)
        for gate in GATE_ORDER:
            nc.vector.memset(wh_scales[gate, 1][:].bitcast(I32), 0)
        nc.vector.memset(mix[:], 0.0)
        for f in range(P // FACTION):
            block = slice(f * FACTION, (f + 1) * FACTION)
            nc.vector.memset(mix[block, block], 3.0)
        nc.vector.tensor_scalar_mul(out=mix_parts[:, 0, :], in0=ident[:], scalar1=544.0)
        nc.vector.tensor_copy(out=mix_parts[:, 1, :], in_=mix[:])
        nc.vector.scalar_tensor_tensor(
            out=mix[:], in0=ident[:], scalar=544.0, in1=mix[:], op0=ALU.mult, op1=ALU.add
        )

        def load_rows(half):
            cols = slice(half * D_HID // 2, (half + 1) * D_HID // 2)
            w_row = w_ih[D_IN : D_IN + 1, :].rearrange("o (g n) -> o g n", g=GATES)
            b_ih_row = b_ih.rearrange("(o g n) -> o g n", o=1, g=GATES)
            b_hh_row = b_hh.rearrange("(o g n) -> o g n", o=1, g=GATES)
            nc.sync.dma_start(out=rows[half][0:1, :, :], in_=w_row[:, :, cols])
            nc.sync.dma_start(out=rows[half][32:33, :, :], in_=b_ih_row[:, :, cols])
            nc.sync.dma_start(out=rows[half][64:65, 0:N, :], in_=b_hh_row[:, 0:N, cols])
            nc.sync.dma_start(out=rows[half][96:97, N:GATES, :], in_=b_hh_row[:, N:GATES, cols])

        for gate in GATE_ORDER:
            if gate != R:
                load_raw(0, gate)
            load_words(0, gate)
            load_scale_rows(gate, 0)
            if gate == R:
                load_raw(0, gate)
            if gate == GATE_ORDER[0]:
                load_rows(0)
                nc.sync.dma_start(
                    out=left[0:1, 0:ROW_TILES, :], in_=tension.rearrange("(o i r) -> o i r", o=1, i=ROW_TILES)
                )

        units = [(c, gate) for c in range(CHUNKS) for gate in GATE_ORDER]

        def load_chunk(c):
            for gate in GATE_ORDER:
                ahead = units.index((c, gate)) + 1
                if ahead < len(units):
                    load_raw(*units[ahead])
                load_scale_rows(gate, c)
                load_words(c, gate)
                if (c, gate) == (1, Z):
                    load_rows(1)

        def transpose_and_quantise(x_sb, g, codes, scales):
            x_words = x_sb[:].bitcast(F32)
            flipped = bank([P, 2, CELLS])
            for i in range(ROW_TILES):
                for u in range(2):
                    nc.tensor.transpose(
                        flipped[:, u, row_tile(i)],
                        x_words[:, i, K_PASS // 2 * g + u : K_PASS // 2 * (g + 1) : 2],
                        ident[:],
                    )
            x_grouped = stream.tile([P, CELLS, PACK], BF16, name="x_grouped", tag="x_grouped", bufs=3, align_bytes=64)
            nc.scalar.copy(out=x_grouped[:].bitcast(F32), in_=flipped[:].rearrange("p u r -> p r u"))
            nc.vector.quantize_mx(
                out=codes[:, g, :].bitcast(FP8X4),
                scales=scales[:, g, :],
                in_=x_grouped[:].rearrange("p r t -> p (r t)"),
            )

        for g in range(HID_PASSES):
            transpose_and_quantise(h_sb, g, h_codes, h_scales)

        both = range(ROW_TILES)
        on_scalar = nc.scalar.copy
        on_vector = nc.vector.tensor_copy

        transpose_and_quantise(eng_sb, 0, eng_codes, eng_scales)
        for i in both:
            hidden_passes(0, i, R, stop=False)
        gate_terms(0, R)
        bias_term(0)
        for half in range(2):
            regroup(0, R, half, on_vector)
        quantise(0, R)
        load_raw(1, R)
        load_chunk(1)

        def gate_r(c):
            for i in both:
                input_pass(acc[c, i, R], c, i, R, start=False)
            for i in both:
                gate_sum(c, i, R)
            for i in both:
                sigmoid(c, i, R, WHOLE)

        last = CHUNKS - 1
        for c in range(CHUNKS):
            more = c + 1 < CHUNKS
            if c > 0 and more:
                load_chunk(c + 1)
            if c > 0:
                for i in both:
                    hidden_passes(c, i, R, stop=False)
                blend(c - 1, [(i, WHOLE) for i in both])
                for half in range(2):
                    regroup(c, Z, half, on_scalar)
            else:
                regroup(0, N, 0, on_vector)
            gate_r(c)
            if c == 0:
                gate_terms(0, Z)
                gate_terms(1, R)
            for i in both:
                hidden_passes(c, i, N, stop=True)
            if c == 0:
                regroup(0, N, 1, on_vector)
                quantise(0, N)
                regroup(0, Z, 0, on_vector)
            elif more:
                regroup(c + 1, R, 0, on_scalar)
            hidden_part(c)
            if c > 0 and more:
                regroup(c + 1, R, 1, on_scalar)
            candidate_matmuls(c)
            if c == 0:
                reset(0)
                regroup(0, Z, 1, on_scalar)
                bias_term(1)
                for half in range(2):
                    regroup(1, R, half, on_scalar)
            quantise(c, Z)
            if c > 0:
                for i in both:
                    mix_factions(c - 1, i, WHOLE)
                reset(c)
                if more:
                    bias_term(c + 1)
            candidate(c)
            if c > 0 and more:
                quantise(c + 1, R)
                regroup(c + 1, N, 0, on_vector)
            candidate_tanh(c)
            for i in both:
                hidden_passes(c, i, Z, stop=False)
                input_pass(acc[c, i, Z], c, i, Z, start=False)
            gate_sum(c, 0, Z)
            if c == 0:
                regroup(1, N, 0, on_scalar)
            if c == last:
                blend_difference(c, 0)
            gate_sum(c, 1, Z)
            if more:
                if c == 0:
                    quantise(1, R)
                    regroup(1, N, 1, on_vector)
                else:
                    regroup(c + 1, N, 1, on_scalar)
                for i in both:
                    blend_difference(c, i)
            for i in both:
                sigmoid(c, i, Z, WHOLE)
            if more:
                if c > 0:
                    gate_terms(c + 1, R)
                gate_terms(c + 1, Z)
                quantise(c + 1, N)
        for i in both:
            for cols in HALVES:
                mix_hiddens(last, i, cols)
        pull(last, [(0, cols) for cols in HALVES])
        blend_difference(last, 1)
        pull(last, [(1, cols) for cols in HALVES])
        for i in both:
            for cols in HALVES:
                mix_part(last, i, cols, start=False)
                scale_and_store(last, i, cols)
